import numpy as np
import ml_dtypes


def mxq(x, axis, fmt="e4m3"):
    dtype, down = {"e4m3": (ml_dtypes.float8_e4m3fn, 7), "e5m2": (ml_dtypes.float8_e5m2, 14)}[fmt]
    v = np.moveaxis(np.asarray(x, np.float32).astype(ml_dtypes.bfloat16).astype(np.float64), axis, -1)
    blocks = v.reshape(v.shape[:-1] + (-1, 32))
    amax = np.abs(blocks).max(-1, keepdims=True)
    byte = np.maximum(np.where(amax > 0, np.frexp(amax)[1] - 1 + 127, 0) - down, 1)
    scale = np.exp2(byte - 127.0)
    codes = (blocks / scale).astype(np.float32).astype(dtype).astype(np.float64)
    return np.moveaxis((codes * scale).reshape(v.shape), -1, axis)


WIDE = False


def mx_kscale(k):
    if not WIDE:
        return np.ones(k)
    levels = np.array([10, -10, 5, -5, 0])
    a = np.random.permutation(np.resize(levels, k // 512 * 4)).reshape(k // 512, 4)
    idx = np.arange(k)
    return np.exp2(a[idx // 512, idx % 128 // 32])


BF16 = ml_dtypes.bfloat16


def bf(x):
    return np.asarray(x, np.float32).astype(BF16)


def f64(x):
    return np.asarray(x).astype(np.float64)


N, E, SD, AD, RD, HID, NH = 384, 7, 120, 8, 8, 512, 3
OD = SD + RD


def swish(v):
    return v * (1.0 / (1.0 + np.exp(-v)))


def softplus(v):
    return np.maximum(v, 0.0) + np.log1p(np.exp(-np.abs(v)))


def soft_clamp_exp(v, hi, lo):
    v = (hi - softplus(hi - 2.0 * v)) / 2.0
    v = (lo + softplus(2.0 * v - lo)) / 2.0
    return np.exp(v)


def setup_inputs():
    ks = mx_kscale(HID)
    return {"h": bf(swish(np.random.standard_normal((N, E, HID))) * ks),
            "Wh": bf(np.random.standard_normal((E, HID, HID)) * 1.6 / np.sqrt(HID) / ks[None, :, None]),
            "bh": bf(np.random.standard_normal((E, HID)) * 0.2),
            "Wmu": bf(np.random.standard_normal((E, HID, OD)) * 1.6 / np.sqrt(HID)),
            "bmu": bf(np.random.standard_normal((E, OD)) * 0.3),
            "Wsig": bf(np.random.standard_normal((E, HID, OD)) * 2.0 / np.sqrt(HID)),
            "bsig": bf(np.random.standard_normal((E, OD)) * 0.3),
            "max_lv_s": bf(0.5 + 0.2 * np.random.standard_normal((1, SD))),
            "min_lv_s": bf(-2.5 + 0.3 * np.random.standard_normal((1, SD))),
            "max_lv_r": bf(0.5 + 0.2 * np.random.standard_normal((1, RD))),
            "min_lv_r": bf(-2.5 + 0.3 * np.random.standard_normal((1, RD)))}


def reference(h, Wh, bh, Wmu, bmu, Wsig, bsig, max_lv_s, min_lv_s, max_lv_r, min_lv_r):
    hq = mxq(f64(h), 2, "e4m3").transpose(1, 0, 2)
    g = swish((hq @ mxq(f64(Wh), 1, "e4m3")) + f64(bh)[:, None, :])
    gq = mxq(g, 2, "e4m3")
    mu = ((gq @ mxq(f64(Wmu), 1, "e4m3")) + f64(bmu)[:, None, :]).transpose(1, 0, 2)
    sigma = ((gq @ mxq(f64(Wsig), 1, "e4m3")) + f64(bsig)[:, None, :]).transpose(1, 0, 2)
    ds_mu, r_mu = mu[..., :SD], mu[..., SD:]
    ds_sg, r_sg = sigma[..., :SD], sigma[..., SD:]
    ds_sg = soft_clamp_exp(ds_sg, f64(max_lv_s), f64(min_lv_s))
    r_sg = soft_clamp_exp(r_sg, f64(max_lv_r), f64(min_lv_r))
    return ds_mu, ds_sg, r_mu, r_sg

@@ -1,0 +1,321 @@
+from contextlib import ExitStack
+
+import concourse.mybir as mybir
+from concourse.masks import make_identity
+
+F32 = mybir.dt.float32
+BF16 = mybir.dt.bfloat16
+U32 = mybir.dt.uint32
+U8 = mybir.dt.uint8
+FP8X4 = mybir.dt.float8_e4m3fn_x4
+ACT = mybir.ActivationFunctionType
+ALU = mybir.AluOpType
+
+P = 128
+N_ROWS = 384
+NCH = N_ROWS // P
+E = 7
+HID = 512
+OD = 128
+SD = 120
+T = 4
+
+FLOPS = 2 * E * N_ROWS * HID * (HID + 2 * OD)
+
+SQRT_GROUPS = ((0, 2), (2, 4), (4, 6), (6, 7))
+
+
+def regroup(engine_copy, dst, src):
+    engine_copy(
+        out=dst.rearrange("p (c i t) -> p c t i", i=4, t=T),
+        in_=src.rearrange("p t (c i) -> p c t i", i=4),
+    )
+
+
+def tile_ensembleenvprob_pa_kernel(
+    tc, h, Wh, bh, Wmu, bmu, Wsig, bsig, max_lv_s, min_lv_s, max_lv_r, min_lv_r,
+    out_0, out_1, out_2, out_3,
+):
+    nc = tc.nc
+    with ExitStack() as ctx:
+        const = ctx.enter_context(tc.tile_pool(name="const", bufs=1))
+        raw = ctx.enter_context(tc.tile_pool(name="raw", bufs=1))
+        grp = ctx.enter_context(tc.tile_pool(name="grp", bufs=2))
+        cod = ctx.enter_context(tc.tile_pool(name="cod", bufs=3))
+        res = ctx.enter_context(tc.tile_pool(name="res", bufs=1))
+        ps_t = ctx.enter_context(tc.psum_pool(name="ps_t", bufs=2))
+        ps_1 = ctx.enter_context(tc.psum_pool(name="ps_1", bufs=4))
+        ps_2 = ctx.enter_context(tc.psum_pool(name="ps_2", bufs=1))
+        ctx.enter_context(tc.manual_schedule())
+
+        ident_f = const.tile([P, P], F32)
+        nc.vector.memset(ident_f[:], 0.0)
+        make_identity(nc, ident_f[:], nomemset=True)
+        rows = const.tile([P, P], BF16)
+        nc.vector.memset(rows[:], 0.0)
+        zrow = const.tile([P, 1024], BF16)
+        nc.vector.memset(zrow[:], 0.0)
+        ones = const.tile([P, P], BF16)
+        nc.vector.memset(ones[:], 1.0)
+        ident_b = const.tile([P, P], BF16)
+        nc.vector.tensor_copy(out=ident_b[:], in_=ident_f[:])
+
+        h_raw = raw.tile([P, NCH, E * HID], BF16)
+        wh_raw = raw.tile([P, E, T, HID], BF16)
+        w2_raw = raw.tile([P, E, T, 2 * OD], BF16)
+        h_view = h.rearrange("(c p) e k -> p c (e k)", p=P)
+
+        def load_h(e0, e1):
+            nc.sync.dma_start(
+                out=h_raw[:, :, e0 * HID : e1 * HID], in_=h_view[:, :, e0 * HID : e1 * HID]
+            )
+
+        def load_wh(e):
+            nc.sync.dma_start(
+                out=wh_raw[:, e].rearrange("p (u r) j -> p u (r j)", u=2),
+                in_=Wh[e].rearrange("(u p r) j -> p u (r j)", u=2, p=P, r=2),
+            )
+
+        def load_w2(e0, e1):
+            for i, w in enumerate((Wmu, Wsig)):
+                nc.sync.dma_start(
+                    out=w2_raw[:, e0:e1, :, i * OD : (i + 1) * OD].rearrange("p e t o -> p (e t) o"),
+                    in_=w[e0:e1].rearrange("e (t p) o -> p (e t) o", p=P),
+                )
+
+        load_h(0, 1)
+        load_wh(0)
+        nc.scalar.dma_start(out=rows[40:41, 0:SD], in_=max_lv_s)
+        nc.scalar.dma_start(out=rows[41:42, 0:SD], in_=min_lv_s)
+        nc.scalar.dma_start(out=rows[42:43, SD:OD], in_=max_lv_r)
+        nc.scalar.dma_start(out=rows[43:44, SD:OD], in_=min_lv_r)
+        nc.scalar.dma_start(out=rows[0 : E * T, :], in_=bh.rearrange("e (t p) -> (e t) p", p=P))
+        nc.scalar.dma_start(out=rows[32 : 32 + E, :], in_=bsig)
+        nc.gpsimd.dma_start(
+            out=zrow[0:1, 0 : E * OD], in_=bmu.rearrange("e o -> (e o)").unsqueeze(0)
+        )
+        load_h(1, 2)
+        load_wh(1)
+        load_w2(0, 1)
+        load_h(2, 3)
+        load_wh(2)
+        load_w2(1, 3)
+        load_h(3, 5)
+        load_wh(3)
+        load_w2(3, 5)
+        load_wh(4)
+        load_h(5, 7)
+        load_wh(5)
+        load_w2(5, 7)
+        load_wh(6)
+
+        rows_ps = ps_t.tile([P, P], BF16, tag="t")
+        nc.tensor.transpose(rows_ps[:], rows[:], ident_b[:])
+        cols = const.tile([P, 44], F32)
+        nc.vector.tensor_copy(out=cols[:], in_=rows_ps[:, 0:44])
+        hl = const.tile([P, 2], F32)
+        nc.vector.tensor_tensor(out=hl[:], in0=cols[:, 40:42], in1=cols[:, 42:44], op=ALU.add)
+        ehl = const.tile([P, 2], F32)
+        nc.scalar.activation(out=ehl[:], in_=hl[:], func=ACT.Exp)
+        half_a = const.tile([P, 1], F32)
+        nc.vector.tensor_scalar(
+            out=half_a[:], in0=ehl[:, 0:1], scalar1=0.5, scalar2=None, op0=ALU.mult
+        )
+        sq_bias = const.tile([P, 1], F32)
+        nc.vector.tensor_tensor(out=sq_bias[:], in0=half_a[:], in1=ehl[:, 1:2], op=ALU.add)
+        neg_half_hi = const.tile([P, 1], F32)
+        nc.vector.tensor_scalar(
+            out=neg_half_hi[:], in0=hl[:, 0:1], scalar1=-0.5, scalar2=None, op0=ALU.mult
+        )
+        th_bias = const.tile([P, E], F32)
+        nc.vector.tensor_scalar(
+            out=th_bias[:], in0=cols[:, 32 : 32 + E], scalar1=neg_half_hi[:, 0:1], scalar2=None,
+            op0=ALU.add,
+        )
+        bmu_bc = const.tile([P, 1024], BF16)
+
+        mu_sb = res.tile([P, NCH, E, OD], F32)
+        sg_sb = res.tile([P, NCH, E, OD], F32)
+        th = res.tile([P, E, N_ROWS], F32)
+        o0 = out_0.rearrange("(c p) e o -> p c e o", p=P)
+        o1 = out_1.rearrange("(c p) e o -> p c e o", p=P)
+        o2 = out_2.rearrange("(c p) e o -> p c e o", p=P)
+        o3 = out_3.rearrange("(c p) e o -> p c e o", p=P)
+
+        h_words = h_raw[:].bitcast(F32)
+        tl = {}
+
+        def quant(codes, scales, grouped, w0, w1):
+            nc.vector.quantize_mx(
+                out=codes[:, w0:w1].bitcast(FP8X4), scales=scales[:, w0:w1],
+                in_=grouped[:, T * w0 : T * w1],
+            )
+
+        def mx(out, lc, ls, l0, rc, rs, r0, n):
+            nc.tensor.matmul_mx(
+                out=out,
+                lhsT=lc[:, l0 : l0 + P].bitcast(FP8X4), lhsT_scale=ls[:, l0 : l0 + P],
+                rhs=rc[:, r0 : r0 + n].bitcast(FP8X4), rhs_scale=rs[:, r0 : r0 + n],
+                start=True, stop=True,
+            )
+
+        def h_transpose(e):
+            t_a = ps_t.tile([P, 2, 2 * P], F32, name="t_a", tag="t")
+            t_b = ps_t.tile([P, 2, P], F32, name="t_b", tag="t")
+            for c in range(NCH):
+                for u in range(2):
+                    dst = t_a[:, u, c * P : (c + 1) * P] if c < 2 else t_b[:, u, :]
+                    w0 = e * (HID // 2) + u * P
+                    nc.tensor.transpose(dst, h_words[:, c, w0 : w0 + P], ident_f[:])
+            hg = grp.tile([P, T * N_ROWS], BF16, name="hg", tag="hg", align_bytes=64)
+            hg_words = hg[:].bitcast(F32)
+            nc.scalar.copy(
+                out=hg_words[:, 0:512].rearrange("p (n u) -> p n u", u=2),
+                in_=t_a[:].rearrange("p u n -> p n u"),
+            )
+            nc.scalar.copy(
+                out=hg_words[:, 512:768].rearrange("p (n u) -> p n u", u=2),
+                in_=t_b[:].rearrange("p u n -> p n u"),
+            )
+            tl["hg", e] = hg
+            tl["hc", e] = cod.tile([P, N_ROWS], U32, name="hc", tag="hc", align_bytes=64)
+            tl["hs", e] = cod.tile([P, N_ROWS], U8, name="hs", tag="hs", align_bytes=64)
+
+        def h_quant(e, part):
+            w0, w1 = ((0, 256), (256, 384))[part]
+            quant(tl["hc", e], tl["hs", e], tl["hg", e], w0, w1)
+
+        def wh_tiles(e):
+            tl["wg", e] = grp.tile([P, T * HID], BF16, name="wg", tag="wg", align_bytes=64)
+            tl["wc", e] = cod.tile([P, HID], U32, name="wc", tag="wc", align_bytes=64)
+            tl["ws", e] = cod.tile([P, HID], U8, name="ws", tag="ws", align_bytes=64)
+
+        def wh_regroup(e, j0, j1):
+            regroup(nc.vector.tensor_copy, tl["wg", e][:, T * j0 : T * j1], wh_raw[:, e, :, j0:j1])
+
+        def wh_quant(e, j0, j1):
+            quant(tl["wc", e], tl["ws", e], tl["wg", e], j0, j1)
+
+        def stage1(e):
+            g_t = grp.tile([P, T, N_ROWS], BF16, name="g_t", tag="g_t")
+            tl["g_t", e] = g_t
+            wc, ws, hc, hs = tl["wc", e], tl["ws", e], tl["hc", e], tl["hs", e]
+            for t in range(T):
+                s1 = ps_1.tile([P, N_ROWS], F32, name="s1", tag="s1")
+                mx(s1[:, 0:256], wc, ws, t * P, hc, hs, 0, 256)
+                mx(s1[:, 256:384], wc, ws, t * P, hc, hs, 256, 128)
+                nc.scalar.activation(
+                    out=g_t[:, t, :], in_=s1[:], func=ACT.Silu,
+                    bias=cols[:, T * e + t : T * e + t + 1], scale=1.0,
+                )
+
+        def w2_regroup(e):
+            w2g = grp.tile([P, T * 2 * OD], BF16, name="w2g", tag="w2g", align_bytes=64)
+            tl["w2g", e] = w2g
+            regroup(nc.scalar.copy, w2g[:], w2_raw[:, e])
+
+        def g_regroup(e):
+            gg = grp.tile([P, T * N_ROWS], BF16, name="gg", tag="gg", align_bytes=64)
+            tl["gg", e] = gg
+            regroup(nc.vector.tensor_copy, gg[:], tl["g_t", e][:])
+
+        def g_quant(e):
+            tl["gc", e] = cod.tile([P, N_ROWS], U32, name="gc", tag="gc", align_bytes=64)
+            tl["gs", e] = cod.tile([P, N_ROWS], U8, name="gs", tag="gs", align_bytes=64)
+            tl["w2c", e] = cod.tile([P, 2 * OD], U32, name="w2c", tag="w2c", align_bytes=64)
+            tl["w2s", e] = cod.tile([P, 2 * OD], U8, name="w2s", tag="w2s", align_bytes=64)
+            quant(tl["gc", e], tl["gs", e], tl["gg", e], 0, 256)
+            quant(tl["gc", e], tl["gs", e], tl["gg", e], 256, 384)
+            quant(tl["w2c", e], tl["w2s", e], tl["w2g", e], 0, 2 * OD)
+
+        def stage2(e):
+            gc, gs, w2c, w2s = tl["gc", e], tl["gs", e], tl["w2c", e], tl["w2s", e]
+            sg_ps = ps_2.tile([P, N_ROWS], F32, name="sg_ps", tag="sg")
+            mx(sg_ps[:, 0:256], w2c, w2s, OD, gc, gs, 0, 256)
+            mx(sg_ps[:, 256:384], w2c, w2s, OD, gc, gs, 256, 128)
+            mu_ps = ps_2.tile([P, NCH, OD], F32, name="mu_ps", tag="mu")
+            for c in range(NCH):
+                mx(mu_ps[:, c, :], gc, gs, c * P, w2c, w2s, 0, OD)
+            tl["sg_ps", e] = sg_ps
+            tl["mu_ps", e] = mu_ps
+
+        def tanh(e):
+            nc.scalar.activation(
+                out=th[:, e, :], in_=tl["sg_ps", e][:], func=ACT.Tanh,
+                bias=th_bias[:, e : e + 1], scale=1.0,
+            )
+
+        def mu_out(e):
+            nc.vector.tensor_tensor(
+                out=mu_sb[:, :, e, :], in0=tl["mu_ps", e][:],
+                in1=bmu_bc[:, e * OD : (e + 1) * OD].unsqueeze(1).to_broadcast([P, NCH, OD]),
+                op=ALU.add,
+            )
+            nc.sync.dma_start(out=o0[:, :, e, :], in_=mu_sb[:, :, e, 0:SD])
+            nc.sync.dma_start(out=o2[:, :, e, :], in_=mu_sb[:, :, e, SD:OD])
+
+        h_transpose(0)
+        wh_tiles(0)
+        wh_regroup(0, 0, 128)
+        wh_regroup(0, 128, 256)
+        h_quant(0, 0)
+        wh_quant(0, 0, 128)
+        h_quant(0, 1)
+        wh_regroup(0, 256, 384)
+        wh_quant(0, 128, 256)
+        wh_regroup(0, 384, 512)
+        wh_quant(0, 256, 384)
+        wh_quant(0, 384, 512)
+
+        for i in range(E):
+            stage1(i)
+            if i + 1 < E:
+                h_transpose(i + 1)
+            if i == 0:
+                bc_ps = ps_t.tile([P, 1024], BF16, tag="t")
+                for k in range(2):
+                    nc.tensor.matmul(
+                        out=bc_ps[:, 512 * k : 512 * (k + 1)], lhsT=ones[:],
+                        rhs=zrow[:, 512 * k : 512 * (k + 1)], start=True, stop=True,
+                    )
+            w2_regroup(i)
+            if i > 0:
+                g_regroup(i - 1)
+            if i + 1 < E:
+                wh_tiles(i + 1)
+                wh_regroup(i + 1, 0, HID)
+            if i > 0:
+                g_quant(i - 1)
+                stage2(i - 1)
+            if i + 1 < E:
+                wh_quant(i + 1, 0, HID)
+                h_quant(i + 1, 0)
+                h_quant(i + 1, 1)
+            if i == 0:
+                nc.vector.tensor_copy(out=bmu_bc[:], in_=bc_ps[:])
+            if 0 < i < E - 1:
+                mu_out(i - 1)
+            if i > 0:
+                tanh(i - 1)
+        g_regroup(E - 1)
+        g_quant(E - 1)
+        mu_out(E - 2)
+        stage2(E - 1)
+        tanh(E - 1)
+        mu_out(E - 1)
+
+        for e0, e1 in SQRT_GROUPS:
+            nc.scalar.activation(
+                out=th[:, e0:e1, :], in_=th[:, e0:e1, :], func=ACT.Sqrt,
+                bias=sq_bias[:, 0:1], scale=half_a[:, 0:1],
+            )
+            for e in range(e0, e1):
+                tp = ps_1.tile([P, NCH, OD], F32, name="tp", tag="s1")
+                for c in range(NCH):
+                    nc.tensor.transpose(tp[:, c, :], th[:, e, c * P : (c + 1) * P], ident_f[:])
+                if e < E - 1:
+                    nc.vector.tensor_copy(out=sg_sb[:, :, e, :], in_=tp[:])
+                else:
+                    nc.scalar.copy(out=sg_sb[:, :, e, :], in_=tp[:])
+                nc.sync.dma_start(out=o1[:, :, e, :], in_=sg_sb[:, :, e, 0:SD])
+                nc.sync.dma_start(out=o3[:, :, e, :], in_=sg_sb[:, :, e, SD:OD])

@@ -19,10 +19,12 @@ HID = 512
 OD = 128
 SD = 120
 T = 4
+LOG2_E = 1.4426950408889634
 
 FLOPS = 2 * E * N_ROWS * HID * (HID + 2 * OD)
 
-SQRT_GROUPS = ((0, 2), (2, 4), (4, 6), (6, 7))
+TP_BANKS = ((0, "t"), (0, "t"), (1, "s1"), (1, "s1"), (1, "s1"), (1, "s1"), (2, "sg"))
+H_GROUPS = ((0, 1), (1, 2), (2, 3), (3, 5), (5, 7))
 
 
 def regroup(engine_copy, dst, src):
@@ -51,24 +53,30 @@ def tile_ensembleenvprob_pa_kernel(
         ident_f = const.tile([P, P], F32)
         nc.vector.memset(ident_f[:], 0.0)
         make_identity(nc, ident_f[:], nomemset=True)
-        rows = const.tile([P, P], BF16)
-        nc.vector.memset(rows[:], 0.0)
+        rows_a = const.tile([P, P], BF16)
+        nc.vector.memset(rows_a[:], 0.0)
+        rows_b = const.tile([P, P], BF16)
+        nc.vector.memset(rows_b[:], 0.0)
         zrow = const.tile([P, 1024], BF16)
         nc.vector.memset(zrow[:], 0.0)
         ones = const.tile([P, P], BF16)
         nc.vector.memset(ones[:], 1.0)
+        twos = const.tile([P, 2], F32)
+        nc.vector.memset(twos[:], 2.0)
         ident_b = const.tile([P, P], BF16)
         nc.vector.tensor_copy(out=ident_b[:], in_=ident_f[:])
 
-        h_raw = raw.tile([P, NCH, E * HID], BF16)
+        h_raw = {}
+        for g0, g1 in H_GROUPS:
+            hr = raw.tile([P, NCH, (g1 - g0) * HID], BF16, name="h_raw%d" % g0, tag="h_raw%d" % g0)
+            for e in range(g0, g1):
+                h_raw[e] = (hr, e - g0)
         wh_raw = raw.tile([P, E, T, HID], BF16)
         w2_raw = raw.tile([P, E, T, 2 * OD], BF16)
         h_view = h.rearrange("(c p) e k -> p c (e k)", p=P)
 
         def load_h(e0, e1):
-            nc.sync.dma_start(
-                out=h_raw[:, :, e0 * HID : e1 * HID], in_=h_view[:, :, e0 * HID : e1 * HID]
-            )
+            nc.sync.dma_start(out=h_raw[e0][0][:], in_=h_view[:, :, e0 * HID : e1 * HID])
 
         def load_wh(e):
             nc.sync.dma_start(
@@ -85,17 +93,19 @@ def tile_ensembleenvprob_pa_kernel(
 
         load_h(0, 1)
         load_wh(0)
-        nc.scalar.dma_start(out=rows[40:41, 0:SD], in_=max_lv_s)
-        nc.scalar.dma_start(out=rows[41:42, 0:SD], in_=min_lv_s)
-        nc.scalar.dma_start(out=rows[42:43, SD:OD], in_=max_lv_r)
-        nc.scalar.dma_start(out=rows[43:44, SD:OD], in_=min_lv_r)
-        nc.scalar.dma_start(out=rows[0 : E * T, :], in_=bh.rearrange("e (t p) -> (e t) p", p=P))
-        nc.scalar.dma_start(out=rows[32 : 32 + E, :], in_=bsig)
-        nc.gpsimd.dma_start(
-            out=zrow[0:1, 0 : E * OD], in_=bmu.rearrange("e o -> (e o)").unsqueeze(0)
-        )
+        nc.scalar.dma_start(out=rows_a[0 : E * T, :], in_=bh.rearrange("e (t p) -> (e t) p", p=P))
+        warm = const.tile([P, 2], F32)
+        nc.scalar.activation(out=warm[:], in_=twos[:], func=ACT.Silu)
+        nc.gpsimd.dma_start(out=rows_b[8:9, 0:SD], in_=max_lv_s)
+        nc.gpsimd.dma_start(out=rows_b[9:10, 0:SD], in_=min_lv_s)
+        nc.gpsimd.dma_start(out=rows_b[10:11, SD:OD], in_=max_lv_r)
+        nc.gpsimd.dma_start(out=rows_b[11:12, SD:OD], in_=min_lv_r)
+        nc.gpsimd.dma_start(out=rows_b[0:E, :], in_=bsig)
         load_h(1, 2)
         load_wh(1)
+        nc.sync.dma_start(
+            out=zrow[0:1, 0 : E * OD], in_=bmu.rearrange("e o -> (e o)").unsqueeze(0)
+        )
         load_w2(0, 1)
         load_h(2, 3)
         load_wh(2)
@@ -109,40 +119,66 @@ def tile_ensembleenvprob_pa_kernel(
         load_w2(5, 7)
         load_wh(6)
 
-        rows_ps = ps_t.tile([P, P], BF16, tag="t")
-        nc.tensor.transpose(rows_ps[:], rows[:], ident_b[:])
-        cols = const.tile([P, 44], F32)
-        nc.vector.tensor_copy(out=cols[:], in_=rows_ps[:, 0:44])
+        cols_a = const.tile([P, E * T], F32)
+        cols_b = const.tile([P, 12], F32)
         hl = const.tile([P, 2], F32)
-        nc.vector.tensor_tensor(out=hl[:], in0=cols[:, 40:42], in1=cols[:, 42:44], op=ALU.add)
+        hl2 = const.tile([P, 2], F32)
         ehl = const.tile([P, 2], F32)
-        nc.scalar.activation(out=ehl[:], in_=hl[:], func=ACT.Exp)
         half_a = const.tile([P, 1], F32)
-        nc.vector.tensor_scalar(
-            out=half_a[:], in0=ehl[:, 0:1], scalar1=0.5, scalar2=None, op0=ALU.mult
-        )
         sq_bias = const.tile([P, 1], F32)
-        nc.vector.tensor_tensor(out=sq_bias[:], in0=half_a[:], in1=ehl[:, 1:2], op=ALU.add)
         neg_half_hi = const.tile([P, 1], F32)
-        nc.vector.tensor_scalar(
-            out=neg_half_hi[:], in0=hl[:, 0:1], scalar1=-0.5, scalar2=None, op0=ALU.mult
-        )
         th_bias = const.tile([P, E], F32)
-        nc.vector.tensor_scalar(
-            out=th_bias[:], in0=cols[:, 32 : 32 + E], scalar1=neg_half_hi[:, 0:1], scalar2=None,
-            op0=ALU.add,
-        )
+
+        def bias_columns():
+            rows_ps = ps_2.tile([P, P], BF16, name="rows_a_ps", tag="mu")
+            nc.tensor.transpose(rows_ps[:], rows_a[:], ident_b[:])
+            nc.vector.tensor_copy(out=cols_a[:], in_=rows_ps[:, 0 : E * T])
+
+        def sigma_transposes():
+            bc_ps = ps_2.tile([P, 1024], BF16, name="bc_ps", tag="sg")
+            for k in range(2):
+                nc.tensor.matmul(
+                    out=bc_ps[:, 512 * k : 512 * (k + 1)], lhsT=ones[:],
+                    rhs=zrow[:, 512 * k : 512 * (k + 1)], start=True, stop=True,
+                )
+            rows_ps = ps_2.tile([P, P], BF16, name="rows_b_ps", tag="mu")
+            nc.tensor.transpose(rows_ps[:], rows_b[:], ident_b[:])
+            return bc_ps, rows_ps
+
+        def sigma_constants(bc_ps, rows_ps):
+            nc.vector.tensor_copy(out=bmu_bc[:], in_=bc_ps[:])
+            nc.vector.tensor_copy(out=cols_b[:], in_=rows_ps[:, 0:12])
+            nc.vector.tensor_tensor(
+                out=hl[:], in0=cols_b[:, 8:10], in1=cols_b[:, 10:12], op=ALU.add
+            )
+            nc.vector.tensor_scalar(
+                out=hl2[:], in0=hl[:], scalar1=LOG2_E, scalar2=None, op0=ALU.mult
+            )
+            nc.gpsimd.tensor_tensor(out=ehl[:], in0=twos[:], in1=hl2[:], op=ALU.pow)
+            nc.vector.tensor_scalar(
+                out=neg_half_hi[:], in0=hl[:, 0:1], scalar1=-0.5, scalar2=None, op0=ALU.mult
+            )
+            nc.vector.tensor_scalar(
+                out=th_bias[:], in0=cols_b[:, 0:E], scalar1=neg_half_hi[:, 0:1], scalar2=None,
+                op0=ALU.add,
+            )
+
+        def sqrt_constants():
+            nc.vector.tensor_scalar(
+                out=half_a[:], in0=ehl[:, 0:1], scalar1=0.5, scalar2=None, op0=ALU.mult
+            )
+            nc.vector.tensor_tensor(out=sq_bias[:], in0=half_a[:], in1=ehl[:, 1:2], op=ALU.add)
+
         bmu_bc = const.tile([P, 1024], BF16)
 
-        mu_sb = res.tile([P, NCH, E, OD], F32)
-        sg_sb = res.tile([P, NCH, E, OD], F32)
+        mu_sb = res.tile([P, E, NCH, OD], F32)
+        sg_sb = res.tile([P, E, NCH, OD], F32)
         th = res.tile([P, E, N_ROWS], F32)
         o0 = out_0.rearrange("(c p) e o -> p c e o", p=P)
         o1 = out_1.rearrange("(c p) e o -> p c e o", p=P)
         o2 = out_2.rearrange("(c p) e o -> p c e o", p=P)
         o3 = out_3.rearrange("(c p) e o -> p c e o", p=P)
 
-        h_words = h_raw[:].bitcast(F32)
         tl = {}
 
         def quant(codes, scales, grouped, w0, w1):
@@ -162,10 +198,11 @@ def tile_ensembleenvprob_pa_kernel(
         def h_transpose(e):
             t_a = ps_t.tile([P, 2, 2 * P], F32, name="t_a", tag="t")
             t_b = ps_t.tile([P, 2, P], F32, name="t_b", tag="t")
+            h_words = h_raw[e][0][:].bitcast(F32)
             for c in range(NCH):
                 for u in range(2):
                     dst = t_a[:, u, c * P : (c + 1) * P] if c < 2 else t_b[:, u, :]
-                    w0 = e * (HID // 2) + u * P
+                    w0 = h_raw[e][1] * (HID // 2) + u * P
                     nc.tensor.transpose(dst, h_words[:, c, w0 : w0 + P], ident_f[:])
             hg = grp.tile([P, T * N_ROWS], BF16, name="hg", tag="hg", align_bytes=64)
             hg_words = hg[:].bitcast(F32)
@@ -190,8 +227,8 @@ def tile_ensembleenvprob_pa_kernel(
             tl["wc", e] = cod.tile([P, HID], U32, name="wc", tag="wc", align_bytes=64)
             tl["ws", e] = cod.tile([P, HID], U8, name="ws", tag="ws", align_bytes=64)
 
-        def wh_regroup(e, j0, j1):
-            regroup(nc.vector.tensor_copy, tl["wg", e][:, T * j0 : T * j1], wh_raw[:, e, :, j0:j1])
+        def wh_regroup(e, j0, j1, engine_copy):
+            regroup(engine_copy, tl["wg", e][:, T * j0 : T * j1], wh_raw[:, e, :, j0:j1])
 
         def wh_quant(e, j0, j1):
             quant(tl["wc", e], tl["ws", e], tl["wg", e], j0, j1)
@@ -206,7 +243,7 @@ def tile_ensembleenvprob_pa_kernel(
                 mx(s1[:, 256:384], wc, ws, t * P, hc, hs, 256, 128)
                 nc.scalar.activation(
                     out=g_t[:, t, :], in_=s1[:], func=ACT.Silu,
-                    bias=cols[:, T * e + t : T * e + t + 1], scale=1.0,
+                    bias=cols_a[:, T * e + t : T * e + t + 1], scale=1.0,
                 )
 
         def w2_regroup(e):
@@ -247,23 +284,24 @@ def tile_ensembleenvprob_pa_kernel(
 
         def mu_out(e):
             nc.vector.tensor_tensor(
-                out=mu_sb[:, :, e, :], in0=tl["mu_ps", e][:],
+                out=mu_sb[:, e], in0=tl["mu_ps", e][:],
                 in1=bmu_bc[:, e * OD : (e + 1) * OD].unsqueeze(1).to_broadcast([P, NCH, OD]),
                 op=ALU.add,
             )
-            nc.sync.dma_start(out=o0[:, :, e, :], in_=mu_sb[:, :, e, 0:SD])
-            nc.sync.dma_start(out=o2[:, :, e, :], in_=mu_sb[:, :, e, SD:OD])
+            nc.sync.dma_start(out=o0[:, :, e, :], in_=mu_sb[:, e, :, 0:SD])
+            nc.sync.dma_start(out=o2[:, :, e, :], in_=mu_sb[:, e, :, SD:OD])
 
         h_transpose(0)
+        bias_columns()
         wh_tiles(0)
-        wh_regroup(0, 0, 128)
-        wh_regroup(0, 128, 256)
+        wh_regroup(0, 0, 128, nc.vector.tensor_copy)
+        wh_regroup(0, 128, 256, nc.vector.tensor_copy)
+        wh_regroup(0, 256, 384, nc.scalar.copy)
+        wh_regroup(0, 384, 512, nc.scalar.copy)
         h_quant(0, 0)
         wh_quant(0, 0, 128)
         h_quant(0, 1)
-        wh_regroup(0, 256, 384)
         wh_quant(0, 128, 256)
-        wh_regroup(0, 384, 512)
         wh_quant(0, 256, 384)
         wh_quant(0, 384, 512)
 
@@ -272,18 +310,13 @@ def tile_ensembleenvprob_pa_kernel(
             if i + 1 < E:
                 h_transpose(i + 1)
             if i == 0:
-                bc_ps = ps_t.tile([P, 1024], BF16, tag="t")
-                for k in range(2):
-                    nc.tensor.matmul(
-                        out=bc_ps[:, 512 * k : 512 * (k + 1)], lhsT=ones[:],
-                        rhs=zrow[:, 512 * k : 512 * (k + 1)], start=True, stop=True,
-                    )
+                bc_ps, rows_ps = sigma_transposes()
             w2_regroup(i)
             if i > 0:
                 g_regroup(i - 1)
             if i + 1 < E:
                 wh_tiles(i + 1)
-                wh_regroup(i + 1, 0, HID)
+                wh_regroup(i + 1, 0, HID, nc.vector.tensor_copy)
             if i > 0:
                 g_quant(i - 1)
                 stage2(i - 1)
@@ -292,7 +325,9 @@ def tile_ensembleenvprob_pa_kernel(
                 h_quant(i + 1, 0)
                 h_quant(i + 1, 1)
             if i == 0:
-                nc.vector.tensor_copy(out=bmu_bc[:], in_=bc_ps[:])
+                sigma_constants(bc_ps, rows_ps)
+            if i == 1:
+                sqrt_constants()
             if 0 < i < E - 1:
                 mu_out(i - 1)
             if i > 0:
@@ -302,20 +337,25 @@ def tile_ensembleenvprob_pa_kernel(
         mu_out(E - 2)
         stage2(E - 1)
         tanh(E - 1)
-        mu_out(E - 1)
 
-        for e0, e1 in SQRT_GROUPS:
-            nc.scalar.activation(
-                out=th[:, e0:e1, :], in_=th[:, e0:e1, :], func=ACT.Sqrt,
-                bias=sq_bias[:, 0:1], scale=half_a[:, 0:1],
+        tp = {}
+
+        def variance(e0, e1):
+            nc.vector.tensor_scalar(
+                out=th[:, e0:e1, :], in0=th[:, e0:e1, :], scalar1=half_a[:, 0:1],
+                scalar2=sq_bias[:, 0:1], op0=ALU.mult, op1=ALU.add,
             )
             for e in range(e0, e1):
-                tp = ps_1.tile([P, NCH, OD], F32, name="tp", tag="s1")
+                pool, tag = TP_BANKS[e]
+                tp[e] = (ps_t, ps_1, ps_2)[pool].tile([P, NCH, OD], F32, name="tp", tag=tag)
                 for c in range(NCH):
-                    nc.tensor.transpose(tp[:, c, :], th[:, e, c * P : (c + 1) * P], ident_f[:])
-                if e < E - 1:
-                    nc.vector.tensor_copy(out=sg_sb[:, :, e, :], in_=tp[:])
-                else:
-                    nc.scalar.copy(out=sg_sb[:, :, e, :], in_=tp[:])
-                nc.sync.dma_start(out=o1[:, :, e, :], in_=sg_sb[:, :, e, 0:SD])
-                nc.sync.dma_start(out=o3[:, :, e, :], in_=sg_sb[:, :, e, SD:OD])
+                    nc.tensor.transpose(tp[e][:, c, :], th[:, e, c * P : (c + 1) * P], ident_f[:])
+
+        variance(0, 3)
+        variance(3, 6)
+        mu_out(E - 1)
+        variance(6, 7)
+        for e in range(E):
+            nc.scalar.activation(out=sg_sb[:, e], in_=tp[e][:], func=ACT.Sqrt)
+            nc.sync.dma_start(out=o1[:, :, e, :], in_=sg_sb[:, e, :, 0:SD])
+            nc.sync.dma_start(out=o3[:, :, e, :], in_=sg_sb[:, e, :, SD:OD])

@@ -18,6 +18,7 @@ E = 7
 HID = 512
 OD = 128
 SD = 120
+RD = 8
 T = 4
 LOG2_E = 1.4426950408889634
 
@@ -96,9 +97,9 @@ def tile_ensembleenvprob_pa_kernel(
         nc.scalar.dma_start(out=rows_a[0 : E * T, :], in_=bh.rearrange("e (t p) -> (e t) p", p=P))
         warm = const.tile([P, 2], F32)
         nc.scalar.activation(out=warm[:], in_=twos[:], func=ACT.Silu)
-        nc.gpsimd.dma_start(out=rows_b[8:9, 0:SD], in_=max_lv_s)
-        nc.gpsimd.dma_start(out=rows_b[9:10, 0:SD], in_=min_lv_s)
-        nc.gpsimd.dma_start(out=rows_b[10:11, SD:OD], in_=max_lv_r)
+        nc.scalar.dma_start(out=rows_b[8:9, 0:SD], in_=max_lv_s)
+        nc.scalar.dma_start(out=rows_b[9:10, 0:SD], in_=min_lv_s)
+        nc.scalar.dma_start(out=rows_b[10:11, SD:OD], in_=max_lv_r)
         nc.gpsimd.dma_start(out=rows_b[11:12, SD:OD], in_=min_lv_r)
         nc.gpsimd.dma_start(out=rows_b[0:E, :], in_=bsig)
         load_h(1, 2)
@@ -174,6 +175,7 @@ def tile_ensembleenvprob_pa_kernel(
         mu_sb = res.tile([P, E, NCH, OD], F32)
         sg_sb = res.tile([P, E, NCH, OD], F32)
         th = res.tile([P, E, N_ROWS], F32)
+        r_pack = res.tile([P, 2, NCH, (E - 1) * RD], F32)
         o0 = out_0.rearrange("(c p) e o -> p c e o", p=P)
         o1 = out_1.rearrange("(c p) e o -> p c e o", p=P)
         o2 = out_2.rearrange("(c p) e o -> p c e o", p=P)
@@ -289,7 +291,16 @@ def tile_ensembleenvprob_pa_kernel(
                 op=ALU.add,
             )
             nc.sync.dma_start(out=o0[:, :, e, :], in_=mu_sb[:, e, :, 0:SD])
-            nc.sync.dma_start(out=o2[:, :, e, :], in_=mu_sb[:, e, :, SD:OD])
+
+        def store_rewards(which, result, out_r):
+            nc.vector.tensor_copy(
+                out=r_pack[:, which].rearrange("p c (e o) -> p e c o", o=RD),
+                in_=result[:, 0 : E - 1, :, SD:OD],
+            )
+            nc.sync.dma_start(
+                out=out_r.rearrange("(c p) e o -> p c (e o)", p=P)[:, :, 0 : (E - 1) * RD],
+                in_=r_pack[:, which],
+            )
 
         h_transpose(0)
         bias_columns()
@@ -355,7 +366,11 @@ def tile_ensembleenvprob_pa_kernel(
         variance(3, 6)
         mu_out(E - 1)
         variance(6, 7)
+        nc.sync.dma_start(out=o2[:, :, E - 1, :], in_=mu_sb[:, E - 1, :, SD:OD])
+        store_rewards(0, mu_sb, out_2)
         for e in range(E):
             nc.scalar.activation(out=sg_sb[:, e], in_=tp[e][:], func=ACT.Sqrt)
             nc.sync.dma_start(out=o1[:, :, e, :], in_=sg_sb[:, e, :, 0:SD])
-            nc.sync.dma_start(out=o3[:, :, e, :], in_=sg_sb[:, e, :, SD:OD])
+            if e == E - 2:
+                store_rewards(1, sg_sb, out_3)
+        nc.sync.dma_start(out=o3[:, :, E - 1, :], in_=sg_sb[:, E - 1, :, SD:OD])

@@ -86,11 +86,12 @@ def tile_ensembleenvprob_pa_kernel(
             )
 
         def load_w2(e0, e1):
-            for i, w in enumerate((Wmu, Wsig)):
-                nc.sync.dma_start(
-                    out=w2_raw[:, e0:e1, :, i * OD : (i + 1) * OD].rearrange("p e t o -> p (e t) o"),
-                    in_=w[e0:e1].rearrange("e (t p) o -> p (e t) o", p=P),
-                )
+            for e in range(e0, e1):
+                for i, w in enumerate((Wmu, Wsig)):
+                    nc.sync.dma_start(
+                        out=w2_raw[:, e, :, i * OD : (i + 1) * OD],
+                        in_=w[e].rearrange("(t p) o -> p t o", p=P),
+                    )
 
         load_h(0, 1)
         load_wh(0)

@@ -105,21 +105,22 @@ def tile_ensembleenvprob_pa_kernel(
         nc.gpsimd.dma_start(out=rows_b[0:E, :], in_=bsig)
         load_h(1, 2)
         load_wh(1)
+        load_h(2, 3)
+        load_wh(2)
         nc.sync.dma_start(
             out=zrow[0:1, 0 : E * OD], in_=bmu.rearrange("e o -> (e o)").unsqueeze(0)
         )
         load_w2(0, 1)
-        load_h(2, 3)
-        load_wh(2)
-        load_w2(1, 3)
         load_h(3, 5)
         load_wh(3)
-        load_w2(3, 5)
+        load_w2(1, 2)
         load_wh(4)
+        load_w2(2, 3)
         load_h(5, 7)
         load_wh(5)
-        load_w2(5, 7)
+        load_w2(3, 4)
         load_wh(6)
+        load_w2(4, 7)
 
         cols_a = const.tile([P, E * T], F32)
         cols_b = const.tile([P, 12], F32)
@@ -316,32 +317,36 @@ def tile_ensembleenvprob_pa_kernel(
         wh_quant(0, 128, 256)
         wh_quant(0, 256, 384)
         wh_quant(0, 384, 512)
+        h_transpose(1)
+        wh_tiles(1)
+        wh_regroup(1, 0, HID, nc.vector.tensor_copy)
 
         for i in range(E):
             stage1(i)
-            if i + 1 < E:
-                h_transpose(i + 1)
+            if i + 2 < E:
+                h_transpose(i + 2)
             if i == 0:
                 bc_ps, rows_ps = sigma_transposes()
             w2_regroup(i)
             if i > 0:
                 g_regroup(i - 1)
             if i + 1 < E:
-                wh_tiles(i + 1)
-                wh_regroup(i + 1, 0, HID, nc.vector.tensor_copy)
-            if i > 0:
-                g_quant(i - 1)
-                stage2(i - 1)
-            if i + 1 < E:
-                wh_quant(i + 1, 0, HID)
                 h_quant(i + 1, 0)
                 h_quant(i + 1, 1)
+                wh_quant(i + 1, 0, HID)
+            if i > 0:
+                g_quant(i - 1)
+            if i > 1:
+                mu_out(i - 2)
+            if i > 0:
+                stage2(i - 1)
             if i == 0:
                 sigma_constants(bc_ps, rows_ps)
             if i == 1:
                 sqrt_constants()
-            if 0 < i < E - 1:
-                mu_out(i - 1)
+            if i + 2 < E:
+                wh_tiles(i + 2)
+                wh_regroup(i + 2, 0, HID, nc.vector.tensor_copy)
             if i > 0:
                 tanh(i - 1)
         g_regroup(E - 1)

@@ -24,7 +24,8 @@ LOG2_E = 1.4426950408889634
 
 FLOPS = 2 * E * N_ROWS * HID * (HID + 2 * OD)
 
-TP_BANKS = ((0, "t"), (0, "t"), (1, "s1"), (1, "s1"), (1, "s1"), (1, "s1"), (2, "sg"))
+W2_STEPS = ((0,), (1,), (2, 3), (4,), (5,), (6,), ())
+HALVES = ((0, 4), (4, E))
 H_GROUPS = ((0, 1), (1, 2), (2, 3), (3, 5), (5, 7))
 
 
@@ -43,29 +44,29 @@ def tile_ensembleenvprob_pa_kernel(
     with ExitStack() as ctx:
         const = ctx.enter_context(tc.tile_pool(name="const", bufs=1))
         raw = ctx.enter_context(tc.tile_pool(name="raw", bufs=1))
-        grp = ctx.enter_context(tc.tile_pool(name="grp", bufs=2))
-        cod = ctx.enter_context(tc.tile_pool(name="cod", bufs=3))
+        grp = ctx.enter_context(tc.tile_pool(name="grp", bufs=3))
+        cod = ctx.enter_context(tc.tile_pool(name="cod", bufs=4))
         res = ctx.enter_context(tc.tile_pool(name="res", bufs=1))
         ps_t = ctx.enter_context(tc.psum_pool(name="ps_t", bufs=2))
         ps_1 = ctx.enter_context(tc.psum_pool(name="ps_1", bufs=4))
         ps_2 = ctx.enter_context(tc.psum_pool(name="ps_2", bufs=1))
         ctx.enter_context(tc.manual_schedule())
 
+        twos = const.tile([P, 2], F32)
+        nc.vector.memset(twos[:], 2.0)
         ident_f = const.tile([P, P], F32)
         nc.vector.memset(ident_f[:], 0.0)
         make_identity(nc, ident_f[:], nomemset=True)
         rows_a = const.tile([P, P], BF16)
-        nc.vector.memset(rows_a[:], 0.0)
+        nc.gpsimd.memset(rows_a[:], 0.0)
+        nc.gpsimd.dma_start(out=rows_a[0 : E * T, :], in_=bh.rearrange("e (t p) -> (e t) p", p=P))
         rows_b = const.tile([P, P], BF16)
         nc.vector.memset(rows_b[:], 0.0)
         zrow = const.tile([P, 1024], BF16)
         nc.vector.memset(zrow[:], 0.0)
         ones = const.tile([P, P], BF16)
         nc.vector.memset(ones[:], 1.0)
-        twos = const.tile([P, 2], F32)
-        nc.vector.memset(twos[:], 2.0)
         ident_b = const.tile([P, P], BF16)
-        nc.vector.tensor_copy(out=ident_b[:], in_=ident_f[:])
 
         h_raw = {}
         for g0, g1 in H_GROUPS:
@@ -93,31 +94,30 @@ def tile_ensembleenvprob_pa_kernel(
                         in_=w[e].rearrange("(t p) o -> p t o", p=P),
                     )
 
-        load_h(0, 1)
         load_wh(0)
-        nc.scalar.dma_start(out=rows_a[0 : E * T, :], in_=bh.rearrange("e (t p) -> (e t) p", p=P))
+        load_h(0, 1)
         warm = const.tile([P, 2], F32)
         nc.scalar.activation(out=warm[:], in_=twos[:], func=ACT.Silu)
-        nc.scalar.dma_start(out=rows_b[8:9, 0:SD], in_=max_lv_s)
-        nc.scalar.dma_start(out=rows_b[9:10, 0:SD], in_=min_lv_s)
-        nc.scalar.dma_start(out=rows_b[10:11, SD:OD], in_=max_lv_r)
-        nc.gpsimd.dma_start(out=rows_b[11:12, SD:OD], in_=min_lv_r)
-        nc.gpsimd.dma_start(out=rows_b[0:E, :], in_=bsig)
-        load_h(1, 2)
         load_wh(1)
-        load_h(2, 3)
+        load_h(1, 2)
+        nc.sync.dma_start(out=rows_b[0:E, :], in_=bsig)
+        nc.sync.dma_start(out=rows_b[8:9, 0:SD], in_=max_lv_s)
+        nc.sync.dma_start(out=rows_b[9:10, 0:SD], in_=min_lv_s)
+        nc.sync.dma_start(out=rows_b[10:11, SD:OD], in_=max_lv_r)
+        nc.sync.dma_start(out=rows_b[11:12, SD:OD], in_=min_lv_r)
         load_wh(2)
+        load_h(2, 3)
         nc.sync.dma_start(
             out=zrow[0:1, 0 : E * OD], in_=bmu.rearrange("e o -> (e o)").unsqueeze(0)
         )
         load_w2(0, 1)
-        load_h(3, 5)
         load_wh(3)
+        load_h(3, 5)
         load_w2(1, 2)
         load_wh(4)
         load_w2(2, 3)
-        load_h(5, 7)
         load_wh(5)
+        load_h(5, 7)
         load_w2(3, 4)
         load_wh(6)
         load_w2(4, 7)
@@ -132,10 +132,12 @@ def tile_ensembleenvprob_pa_kernel(
         neg_half_hi = const.tile([P, 1], F32)
         th_bias = const.tile([P, E], F32)
 
+        def bias_transpose():
+            tl["rows_ps"] = ps_2.tile([P, P], BF16, name="rows_a_ps", tag="mu")
+            nc.tensor.transpose(tl["rows_ps"][:], rows_a[:], ident_b[:])
+
         def bias_columns():
-            rows_ps = ps_2.tile([P, P], BF16, name="rows_a_ps", tag="mu")
-            nc.tensor.transpose(rows_ps[:], rows_a[:], ident_b[:])
-            nc.vector.tensor_copy(out=cols_a[:], in_=rows_ps[:, 0 : E * T])
+            nc.scalar.copy(out=cols_a[:], in_=tl["rows_ps"][:, 0 : E * T])
 
         def sigma_transposes():
             bc_ps = ps_2.tile([P, 1024], BF16, name="bc_ps", tag="sg")
@@ -149,35 +151,38 @@ def tile_ensembleenvprob_pa_kernel(
             return bc_ps, rows_ps
 
         def sigma_constants(bc_ps, rows_ps):
-            nc.vector.tensor_copy(out=bmu_bc[:], in_=bc_ps[:])
-            nc.vector.tensor_copy(out=cols_b[:], in_=rows_ps[:, 0:12])
-            nc.vector.tensor_tensor(
+            nc.scalar.copy(out=cols_b[:], in_=rows_ps[:, 0:12])
+            for k in range(2):
+                nc.scalar.copy(
+                    out=bmu_bc[:, 512 * k : 512 * (k + 1)], in_=bc_ps[:, 512 * k : 512 * (k + 1)]
+                )
+            nc.gpsimd.tensor_tensor(
                 out=hl[:], in0=cols_b[:, 8:10], in1=cols_b[:, 10:12], op=ALU.add
             )
-            nc.vector.tensor_scalar(
+            nc.gpsimd.tensor_scalar(
                 out=hl2[:], in0=hl[:], scalar1=LOG2_E, scalar2=None, op0=ALU.mult
             )
             nc.gpsimd.tensor_tensor(out=ehl[:], in0=twos[:], in1=hl2[:], op=ALU.pow)
-            nc.vector.tensor_scalar(
+            nc.gpsimd.tensor_scalar(
                 out=neg_half_hi[:], in0=hl[:, 0:1], scalar1=-0.5, scalar2=None, op0=ALU.mult
             )
-            nc.vector.tensor_scalar(
+            nc.gpsimd.tensor_scalar(
                 out=th_bias[:], in0=cols_b[:, 0:E], scalar1=neg_half_hi[:, 0:1], scalar2=None,
                 op0=ALU.add,
             )
 
-        def sqrt_constants():
-            nc.vector.tensor_scalar(
+            nc.gpsimd.tensor_scalar(
                 out=half_a[:], in0=ehl[:, 0:1], scalar1=0.5, scalar2=None, op0=ALU.mult
             )
-            nc.vector.tensor_tensor(out=sq_bias[:], in0=half_a[:], in1=ehl[:, 1:2], op=ALU.add)
+            nc.gpsimd.tensor_tensor(out=sq_bias[:], in0=half_a[:], in1=ehl[:, 1:2], op=ALU.add)
 
         bmu_bc = const.tile([P, 1024], BF16)
 
         mu_sb = res.tile([P, E, NCH, OD], F32)
-        sg_sb = res.tile([P, E, NCH, OD], F32)
+        sg_s = res.tile([P, NCH, E, SD], F32)
+        sg_r = res.tile([P, NCH, E, RD], F32)
         th = res.tile([P, E, N_ROWS], F32)
-        r_pack = res.tile([P, 2, NCH, (E - 1) * RD], F32)
+        mu_r = res.tile([P, NCH, E, RD], F32)
         o0 = out_0.rearrange("(c p) e o -> p c e o", p=P)
         o1 = out_1.rearrange("(c p) e o -> p c e o", p=P)
         o2 = out_2.rearrange("(c p) e o -> p c e o", p=P)
@@ -249,6 +254,8 @@ def tile_ensembleenvprob_pa_kernel(
                     out=g_t[:, t, :], in_=s1[:], func=ACT.Silu,
                     bias=cols_a[:, T * e + t : T * e + t + 1], scale=1.0,
                 )
+                if t == 1 and e > 1:
+                    tanh(e - 2)
 
         def w2_regroup(e):
             w2g = grp.tile([P, T * 2 * OD], BF16, name="w2g", tag="w2g", align_bytes=64)
@@ -260,24 +267,31 @@ def tile_ensembleenvprob_pa_kernel(
             tl["gg", e] = gg
             regroup(nc.vector.tensor_copy, gg[:], tl["g_t", e][:])
 
-        def g_quant(e):
+        def g_tiles(e):
             tl["gc", e] = cod.tile([P, N_ROWS], U32, name="gc", tag="gc", align_bytes=64)
             tl["gs", e] = cod.tile([P, N_ROWS], U8, name="gs", tag="gs", align_bytes=64)
             tl["w2c", e] = cod.tile([P, 2 * OD], U32, name="w2c", tag="w2c", align_bytes=64)
             tl["w2s", e] = cod.tile([P, 2 * OD], U8, name="w2s", tag="w2s", align_bytes=64)
+
+        def g_quant(e):
             quant(tl["gc", e], tl["gs", e], tl["gg", e], 0, 256)
             quant(tl["gc", e], tl["gs", e], tl["gg", e], 256, 384)
+
+        def w2_quant(e):
             quant(tl["w2c", e], tl["w2s", e], tl["w2g", e], 0, 2 * OD)
 
-        def stage2(e):
+        def stage2_sigma(e):
             gc, gs, w2c, w2s = tl["gc", e], tl["gs", e], tl["w2c", e], tl["w2s", e]
             sg_ps = ps_2.tile([P, N_ROWS], F32, name="sg_ps", tag="sg")
             mx(sg_ps[:, 0:256], w2c, w2s, OD, gc, gs, 0, 256)
             mx(sg_ps[:, 256:384], w2c, w2s, OD, gc, gs, 256, 128)
+            tl["sg_ps", e] = sg_ps
+
+        def stage2_mu(e):
+            gc, gs, w2c, w2s = tl["gc", e], tl["gs", e], tl["w2c", e], tl["w2s", e]
             mu_ps = ps_2.tile([P, NCH, OD], F32, name="mu_ps", tag="mu")
             for c in range(NCH):
                 mx(mu_ps[:, c, :], gc, gs, c * P, w2c, w2s, 0, OD)
-            tl["sg_ps", e] = sg_ps
             tl["mu_ps", e] = mu_ps
 
         def tanh(e):
@@ -294,68 +308,72 @@ def tile_ensembleenvprob_pa_kernel(
             )
             nc.sync.dma_start(out=o0[:, :, e, :], in_=mu_sb[:, e, :, 0:SD])
 
-        def store_rewards(which, result, out_r):
-            nc.vector.tensor_copy(
-                out=r_pack[:, which].rearrange("p c (e o) -> p e c o", o=RD),
-                in_=result[:, 0 : E - 1, :, SD:OD],
-            )
-            nc.sync.dma_start(
-                out=out_r.rearrange("(c p) e o -> p c (e o)", p=P)[:, :, 0 : (E - 1) * RD],
-                in_=r_pack[:, which],
-            )
-
-        h_transpose(0)
-        bias_columns()
         wh_tiles(0)
-        wh_regroup(0, 0, 128, nc.vector.tensor_copy)
-        wh_regroup(0, 128, 256, nc.vector.tensor_copy)
-        wh_regroup(0, 256, 384, nc.scalar.copy)
-        wh_regroup(0, 384, 512, nc.scalar.copy)
-        h_quant(0, 0)
-        wh_quant(0, 0, 128)
-        h_quant(0, 1)
-        wh_quant(0, 128, 256)
-        wh_quant(0, 256, 384)
-        wh_quant(0, 384, 512)
-        h_transpose(1)
+        wh_regroup(0, 0, 256, nc.vector.tensor_copy)
+        wh_regroup(0, 256, 512, nc.vector.tensor_copy)
+        nc.vector.tensor_copy(out=ident_b[:], in_=ident_f[:])
+        h_transpose(0)
+        bias_transpose()
+        wh_quant(0, 0, 256)
+        wh_quant(0, 256, 512)
         wh_tiles(1)
-        wh_regroup(1, 0, HID, nc.vector.tensor_copy)
+        wh_regroup(1, 0, 256, nc.vector.tensor_copy)
+        h_quant(0, 0)
+        h_quant(0, 1)
+        bias_columns()
+        wh_regroup(1, 256, 512, nc.vector.tensor_copy)
+        wh_quant(1, 0, HID)
+        wh_tiles(2)
+        wh_regroup(2, 0, HID, nc.vector.tensor_copy)
 
         for i in range(E):
             stage1(i)
+            if i == 0:
+                h_transpose(1)
+                h_quant(1, 0)
+                h_quant(1, 1)
             if i + 2 < E:
                 h_transpose(i + 2)
             if i == 0:
                 bc_ps, rows_ps = sigma_transposes()
-            w2_regroup(i)
+            for e in W2_STEPS[i]:
+                w2_regroup(e)
             if i > 0:
                 g_regroup(i - 1)
-            if i + 1 < E:
-                h_quant(i + 1, 0)
-                h_quant(i + 1, 1)
-                wh_quant(i + 1, 0, HID)
+                g_tiles(i - 1)
+            if i + 2 < E:
+                wh_quant(i + 2, 0, HID)
             if i > 0:
                 g_quant(i - 1)
+                w2_quant(i - 1)
             if i > 1:
                 mu_out(i - 2)
             if i > 0:
-                stage2(i - 1)
+                stage2_sigma(i - 1)
+                stage2_mu(i - 1)
             if i == 0:
                 sigma_constants(bc_ps, rows_ps)
-            if i == 1:
-                sqrt_constants()
             if i + 2 < E:
-                wh_tiles(i + 2)
-                wh_regroup(i + 2, 0, HID, nc.vector.tensor_copy)
-            if i > 0:
-                tanh(i - 1)
+                h_quant(i + 2, 0)
+                h_quant(i + 2, 1)
+            if i + 3 < E:
+                wh_tiles(i + 3)
+                wh_regroup(i + 3, 0, HID, nc.vector.tensor_copy)
+        tanh(E - 2)
+        g_tiles(E - 1)
+        w2_quant(E - 1)
         g_regroup(E - 1)
         g_quant(E - 1)
+        stage2_sigma(E - 1)
         mu_out(E - 2)
-        stage2(E - 1)
+        stage2_mu(E - 1)
         tanh(E - 1)
 
         tp = {}
+        for half in range(2):
+            for c in range(NCH):
+                pool, tag = (ps_t, "t") if half == 0 and c < 2 else (ps_1, "s1")
+                tp[half, c] = pool.tile([P, 4, OD], F32, name="tp", tag=tag)
 
         def variance(e0, e1):
             nc.vector.tensor_scalar(
@@ -363,20 +381,33 @@ def tile_ensembleenvprob_pa_kernel(
                 scalar2=sq_bias[:, 0:1], op0=ALU.mult, op1=ALU.add,
             )
             for e in range(e0, e1):
-                pool, tag = TP_BANKS[e]
-                tp[e] = (ps_t, ps_1, ps_2)[pool].tile([P, NCH, OD], F32, name="tp", tag=tag)
+                half = 0 if e < HALVES[0][1] else 1
                 for c in range(NCH):
-                    nc.tensor.transpose(tp[e][:, c, :], th[:, e, c * P : (c + 1) * P], ident_f[:])
+                    nc.tensor.transpose(
+                        tp[half, c][:, e - HALVES[half][0], :], th[:, e, c * P : (c + 1) * P],
+                        ident_f[:],
+                    )
 
-        variance(0, 3)
-        variance(3, 6)
+        def root(half):
+            e0, e1 = HALVES[half]
+            for c in range(NCH):
+                nc.scalar.activation(
+                    out=sg_r[:, c, e0:e1, :], in_=tp[half, c][:, 0 : e1 - e0, SD:OD], func=ACT.Sqrt
+                )
+                if half == 1 and c == NCH - 1:
+                    nc.sync.dma_start(out=o3, in_=sg_r[:])
+                nc.scalar.activation(
+                    out=sg_s[:, c, e0:e1, :], in_=tp[half, c][:, 0 : e1 - e0, 0:SD], func=ACT.Sqrt
+                )
+                nc.sync.dma_start(out=o1[:, c, e0:e1, :], in_=sg_s[:, c, e0:e1, :])
+
+        variance(0, 4)
+        variance(4, E - 1)
         mu_out(E - 1)
-        variance(6, 7)
-        nc.sync.dma_start(out=o2[:, :, E - 1, :], in_=mu_sb[:, E - 1, :, SD:OD])
-        store_rewards(0, mu_sb, out_2)
-        for e in range(E):
-            nc.scalar.activation(out=sg_sb[:, e], in_=tp[e][:], func=ACT.Sqrt)
-            nc.sync.dma_start(out=o1[:, :, e, :], in_=sg_sb[:, e, :, 0:SD])
-            if e == E - 2:
-                store_rewards(1, sg_sb, out_3)
-        nc.sync.dma_start(out=o3[:, :, E - 1, :], in_=sg_sb[:, E - 1, :, SD:OD])
+        variance(E - 1, E)
+        nc.vector.tensor_copy(
+            out=mu_r[:].rearrange("p c e o -> p e c o"), in_=mu_sb[:, :, :, SD:OD]
+        )
+        nc.sync.dma_start(out=o2, in_=mu_r[:])
+        root(0)
+        root(1)

@@ -54,12 +54,12 @@ def tile_ensembleenvprob_pa_kernel(
 
         twos = const.tile([P, 2], F32)
         nc.vector.memset(twos[:], 2.0)
+        rows_a = const.tile([P, P], BF16)
+        nc.vector.memset(rows_a[:], 0.0)
+        nc.scalar.dma_start(out=rows_a[0 : E * T, :], in_=bh.rearrange("e (t p) -> (e t) p", p=P))
         ident_f = const.tile([P, P], F32)
         nc.vector.memset(ident_f[:], 0.0)
         make_identity(nc, ident_f[:], nomemset=True)
-        rows_a = const.tile([P, P], BF16)
-        nc.gpsimd.memset(rows_a[:], 0.0)
-        nc.gpsimd.dma_start(out=rows_a[0 : E * T, :], in_=bh.rearrange("e (t p) -> (e t) p", p=P))
         rows_b = const.tile([P, P], BF16)
         nc.vector.memset(rows_b[:], 0.0)
         zrow = const.tile([P, 1024], BF16)
@@ -129,7 +129,6 @@ def tile_ensembleenvprob_pa_kernel(
         ehl = const.tile([P, 2], F32)
         half_a = const.tile([P, 1], F32)
         sq_bias = const.tile([P, 1], F32)
-        neg_half_hi = const.tile([P, 1], F32)
         th_bias = const.tile([P, E], F32)
 
         def bias_transpose():
@@ -156,25 +155,26 @@ def tile_ensembleenvprob_pa_kernel(
                 nc.scalar.copy(
                     out=bmu_bc[:, 512 * k : 512 * (k + 1)], in_=bc_ps[:, 512 * k : 512 * (k + 1)]
                 )
-            nc.gpsimd.tensor_tensor(
+            nc.vector.tensor_tensor(
                 out=hl[:], in0=cols_b[:, 8:10], in1=cols_b[:, 10:12], op=ALU.add
             )
-            nc.gpsimd.tensor_scalar(
+            nc.vector.tensor_scalar(
                 out=hl2[:], in0=hl[:], scalar1=LOG2_E, scalar2=None, op0=ALU.mult
             )
             nc.gpsimd.tensor_tensor(out=ehl[:], in0=twos[:], in1=hl2[:], op=ALU.pow)
-            nc.gpsimd.tensor_scalar(
-                out=neg_half_hi[:], in0=hl[:, 0:1], scalar1=-0.5, scalar2=None, op0=ALU.mult
-            )
-            nc.gpsimd.tensor_scalar(
-                out=th_bias[:], in0=cols_b[:, 0:E], scalar1=neg_half_hi[:, 0:1], scalar2=None,
-                op0=ALU.add,
+            nc.vector.scalar_tensor_tensor(
+                out=th_bias[:], in0=hl[:, 0:1].to_broadcast([P, E]), scalar=-0.5,
+                in1=cols_b[:, 0:E], op0=ALU.mult, op1=ALU.add,
             )
 
-            nc.gpsimd.tensor_scalar(
+        def sqrt_constants():
+            nc.vector.tensor_scalar(
                 out=half_a[:], in0=ehl[:, 0:1], scalar1=0.5, scalar2=None, op0=ALU.mult
             )
-            nc.gpsimd.tensor_tensor(out=sq_bias[:], in0=half_a[:], in1=ehl[:, 1:2], op=ALU.add)
+            nc.vector.scalar_tensor_tensor(
+                out=sq_bias[:], in0=ehl[:, 0:1], scalar=0.5, in1=ehl[:, 1:2],
+                op0=ALU.mult, op1=ALU.add,
+            )
 
         bmu_bc = const.tile([P, 1024], BF16)
 
@@ -353,6 +353,8 @@ def tile_ensembleenvprob_pa_kernel(
                 stage2_mu(i - 1)
             if i == 0:
                 sigma_constants(bc_ps, rows_ps)
+            if i == 2:
+                sqrt_constants()
             if i + 2 < E:
                 h_quant(i + 2, 0)
                 h_quant(i + 2, 1)

@@ -24,7 +24,6 @@ LOG2_E = 1.4426950408889634
 
 FLOPS = 2 * E * N_ROWS * HID * (HID + 2 * OD)
 
-W2_STEPS = ((0,), (1,), (2, 3), (4,), (5,), (6,), ())
 HALVES = ((0, 4), (4, E))
 H_GROUPS = ((0, 1), (1, 2), (2, 3), (3, 5), (5, 7))
 
@@ -56,7 +55,6 @@ def tile_ensembleenvprob_pa_kernel(
         nc.vector.memset(twos[:], 2.0)
         rows_a = const.tile([P, P], BF16)
         nc.vector.memset(rows_a[:], 0.0)
-        nc.scalar.dma_start(out=rows_a[0 : E * T, :], in_=bh.rearrange("e (t p) -> (e t) p", p=P))
         ident_f = const.tile([P, P], F32)
         nc.vector.memset(ident_f[:], 0.0)
         make_identity(nc, ident_f[:], nomemset=True)
@@ -95,32 +93,34 @@ def tile_ensembleenvprob_pa_kernel(
                     )
 
         load_wh(0)
+        nc.sync.dma_start(out=rows_a[0 : E * T, :], in_=bh.rearrange("e (t p) -> (e t) p", p=P))
         load_h(0, 1)
         warm = const.tile([P, 2], F32)
         nc.scalar.activation(out=warm[:], in_=twos[:], func=ACT.Silu)
         load_wh(1)
         load_h(1, 2)
+        load_w2(0, 1)
+        load_wh(2)
+        load_h(2, 3)
         nc.sync.dma_start(out=rows_b[0:E, :], in_=bsig)
         nc.sync.dma_start(out=rows_b[8:9, 0:SD], in_=max_lv_s)
         nc.sync.dma_start(out=rows_b[9:10, 0:SD], in_=min_lv_s)
         nc.sync.dma_start(out=rows_b[10:11, SD:OD], in_=max_lv_r)
         nc.sync.dma_start(out=rows_b[11:12, SD:OD], in_=min_lv_r)
-        load_wh(2)
-        load_h(2, 3)
         nc.sync.dma_start(
             out=zrow[0:1, 0 : E * OD], in_=bmu.rearrange("e o -> (e o)").unsqueeze(0)
         )
-        load_w2(0, 1)
+        load_w2(1, 2)
         load_wh(3)
         load_h(3, 5)
-        load_w2(1, 2)
-        load_wh(4)
         load_w2(2, 3)
+        load_wh(4)
+        load_w2(3, 4)
         load_wh(5)
         load_h(5, 7)
-        load_w2(3, 4)
+        load_w2(4, 5)
         load_wh(6)
-        load_w2(4, 7)
+        load_w2(5, 7)
 
         cols_a = const.tile([P, E * T], F32)
         cols_b = const.tile([P, 12], F32)
@@ -242,7 +242,7 @@ def tile_ensembleenvprob_pa_kernel(
         def wh_quant(e, j0, j1):
             quant(tl["wc", e], tl["ws", e], tl["wg", e], j0, j1)
 
-        def stage1(e):
+        def stage1(e, between=None):
             g_t = grp.tile([P, T, N_ROWS], BF16, name="g_t", tag="g_t")
             tl["g_t", e] = g_t
             wc, ws, hc, hs = tl["wc", e], tl["ws", e], tl["hc", e], tl["hs", e]
@@ -254,13 +254,13 @@ def tile_ensembleenvprob_pa_kernel(
                     out=g_t[:, t, :], in_=s1[:], func=ACT.Silu,
                     bias=cols_a[:, T * e + t : T * e + t + 1], scale=1.0,
                 )
-                if t == 1 and e > 1:
-                    tanh(e - 2)
+                if t == 1 and between is not None:
+                    between()
 
-        def w2_regroup(e):
+        def w2_regroup(e, engine_copy=nc.scalar.copy):
             w2g = grp.tile([P, T * 2 * OD], BF16, name="w2g", tag="w2g", align_bytes=64)
             tl["w2g", e] = w2g
-            regroup(nc.scalar.copy, w2g[:], w2_raw[:, e])
+            regroup(engine_copy, w2g[:], w2_raw[:, e])
 
         def g_regroup(e):
             gg = grp.tile([P, T * N_ROWS], BF16, name="gg", tag="gg", align_bytes=64)
@@ -289,7 +289,8 @@ def tile_ensembleenvprob_pa_kernel(
 
         def stage2_mu(e):
             gc, gs, w2c, w2s = tl["gc", e], tl["gs", e], tl["w2c", e], tl["w2s", e]
-            mu_ps = ps_2.tile([P, NCH, OD], F32, name="mu_ps", tag="mu")
+            pool, tag = (ps_t, "t") if e in (E - 3, E - 2) else (ps_2, "mu")
+            mu_ps = pool.tile([P, NCH, OD], F32, name="mu_ps", tag=tag)
             for c in range(NCH):
                 mx(mu_ps[:, c, :], gc, gs, c * P, w2c, w2s, 0, OD)
             tl["mu_ps", e] = mu_ps
@@ -323,71 +324,75 @@ def tile_ensembleenvprob_pa_kernel(
         bias_columns()
         wh_regroup(1, 256, 512, nc.vector.tensor_copy)
         wh_quant(1, 0, HID)
-        wh_tiles(2)
-        wh_regroup(2, 0, HID, nc.vector.tensor_copy)
 
-        for i in range(E):
-            stage1(i)
-            if i == 0:
-                h_transpose(1)
-                h_quant(1, 0)
-                h_quant(1, 1)
-            if i + 2 < E:
-                h_transpose(i + 2)
-            if i == 0:
+        stage1(0, lambda: h_transpose(1))
+        h_quant(1, 0)
+        h_quant(1, 1)
+        w2_regroup(0)
+
+        for i in range(1, E - 2):
+            stage1(i, (lambda: tanh(i - 2)) if i > 1 else None)
+            h_transpose(i + 1)
+            if i == 1:
                 bc_ps, rows_ps = sigma_transposes()
-            for e in W2_STEPS[i]:
-                w2_regroup(e)
-            if i > 0:
-                g_regroup(i - 1)
-                g_tiles(i - 1)
-            if i + 2 < E:
-                wh_quant(i + 2, 0, HID)
-            if i > 0:
-                g_quant(i - 1)
-                w2_quant(i - 1)
+            w2_regroup(i)
+            if i == E - 3:
+                h_transpose(E - 1)
+                w2_regroup(E - 2)
+            g_regroup(i - 1)
+            g_tiles(i - 1)
+            wh_tiles(i + 1)
+            wh_regroup(i + 1, 0, HID, nc.vector.tensor_copy)
             if i > 1:
                 mu_out(i - 2)
-            if i > 0:
-                stage2_sigma(i - 1)
-                stage2_mu(i - 1)
-            if i == 0:
+            g_quant(i - 1)
+            w2_quant(i - 1)
+            stage2_sigma(i - 1)
+            stage2_mu(i - 1)
+            if i == 1:
                 sigma_constants(bc_ps, rows_ps)
+            wh_quant(i + 1, 0, HID)
+            h_quant(i + 1, 0)
+            h_quant(i + 1, 1)
             if i == 2:
                 sqrt_constants()
-            if i + 2 < E:
-                h_quant(i + 2, 0)
-                h_quant(i + 2, 1)
-            if i + 3 < E:
-                wh_tiles(i + 3)
-                wh_regroup(i + 3, 0, HID, nc.vector.tensor_copy)
-        tanh(E - 2)
-        g_tiles(E - 1)
-        w2_quant(E - 1)
-        g_regroup(E - 1)
-        g_quant(E - 1)
-        stage2_sigma(E - 1)
-        mu_out(E - 2)
-        stage2_mu(E - 1)
-        tanh(E - 1)
+            if i == E - 3:
+                wh_tiles(E - 1)
+                wh_regroup(E - 1, 0, HID, nc.vector.tensor_copy)
+
+        stage1(E - 2, lambda: tanh(E - 4))
+        h_quant(E - 1, 0)
+        h_quant(E - 1, 1)
+        wh_quant(E - 1, 0, HID)
+        stage1(E - 1)
+        for i in range(E - 3, E):
+            g_tiles(i)
+            g_regroup(i)
+            if i == E - 2:
+                w2_regroup(E - 1, nc.vector.tensor_copy)
+            w2_quant(i)
+            g_quant(i)
+            stage2_sigma(i)
+            if i < E - 1:
+                stage2_mu(i)
+                tanh(i)
 
         tp = {}
-        for half in range(2):
-            for c in range(NCH):
-                pool, tag = (ps_t, "t") if half == 0 and c < 2 else (ps_1, "s1")
-                tp[half, c] = pool.tile([P, 4, OD], F32, name="tp", tag=tag)
 
         def variance(e0, e1):
             nc.vector.tensor_scalar(
                 out=th[:, e0:e1, :], in0=th[:, e0:e1, :], scalar1=half_a[:, 0:1],
                 scalar2=sq_bias[:, 0:1], op0=ALU.mult, op1=ALU.add,
             )
-            for e in range(e0, e1):
-                half = 0 if e < HALVES[0][1] else 1
-                for c in range(NCH):
+
+        def turn(half):
+            e0, e1 = HALVES[half]
+            for c in range(NCH):
+                pool, tag = (ps_t, "t") if half == 1 and c > 0 else (ps_1, "s1")
+                tp[half, c] = pool.tile([P, 4, OD], F32, name="tp", tag=tag)
+                for e in range(e0, e1):
                     nc.tensor.transpose(
-                        tp[half, c][:, e - HALVES[half][0], :], th[:, e, c * P : (c + 1) * P],
-                        ident_f[:],
+                        tp[half, c][:, e - e0, :], th[:, e, c * P : (c + 1) * P], ident_f[:]
                     )
 
         def root(half):
@@ -404,12 +409,19 @@ def tile_ensembleenvprob_pa_kernel(
                 nc.sync.dma_start(out=o1[:, c, e0:e1, :], in_=sg_s[:, c, e0:e1, :])
 
         variance(0, 4)
+        turn(0)
+        mu_out(E - 4)
+        stage2_mu(E - 1)
+        mu_out(E - 3)
+        mu_out(E - 2)
+        tanh(E - 1)
         variance(4, E - 1)
-        mu_out(E - 1)
         variance(E - 1, E)
+        turn(1)
+        root(0)
+        mu_out(E - 1)
         nc.vector.tensor_copy(
             out=mu_r[:].rearrange("p c e o -> p e c o"), in_=mu_sb[:, :, :, SD:OD]
         )
         nc.sync.dma_start(out=o2, in_=mu_r[:])
-        root(0)
         root(1)

@@ -138,7 +138,7 @@ def tile_ensembleenvprob_pa_kernel(
         def bias_columns():
             nc.scalar.copy(out=cols_a[:], in_=tl["rows_ps"][:, 0 : E * T])
 
-        def sigma_transposes():
+        def sigma_vectors():
             bc_ps = ps_2.tile([P, 1024], BF16, name="bc_ps", tag="sg")
             for k in range(2):
                 nc.tensor.matmul(
@@ -147,14 +147,13 @@ def tile_ensembleenvprob_pa_kernel(
                 )
             rows_ps = ps_2.tile([P, P], BF16, name="rows_b_ps", tag="mu")
             nc.tensor.transpose(rows_ps[:], rows_b[:], ident_b[:])
-            return bc_ps, rows_ps
-
-        def sigma_constants(bc_ps, rows_ps):
             nc.scalar.copy(out=cols_b[:], in_=rows_ps[:, 0:12])
             for k in range(2):
                 nc.scalar.copy(
                     out=bmu_bc[:, 512 * k : 512 * (k + 1)], in_=bc_ps[:, 512 * k : 512 * (k + 1)]
                 )
+
+        def tanh_constants():
             nc.vector.tensor_tensor(
                 out=hl[:], in0=cols_b[:, 8:10], in1=cols_b[:, 10:12], op=ALU.add
             )
@@ -332,9 +331,9 @@ def tile_ensembleenvprob_pa_kernel(
 
         for i in range(1, E - 2):
             stage1(i, (lambda: tanh(i - 2)) if i > 1 else None)
-            h_transpose(i + 1)
             if i == 1:
-                bc_ps, rows_ps = sigma_transposes()
+                sigma_vectors()
+            h_transpose(i + 1)
             w2_regroup(i)
             if i == E - 3:
                 h_transpose(E - 1)
@@ -350,7 +349,7 @@ def tile_ensembleenvprob_pa_kernel(
             stage2_sigma(i - 1)
             stage2_mu(i - 1)
             if i == 1:
-                sigma_constants(bc_ps, rows_ps)
+                tanh_constants()
             wh_quant(i + 1, 0, HID)
             h_quant(i + 1, 0)
             h_quant(i + 1, 1)

@@ -60,7 +60,7 @@ def tile_ensembleenvprob_pa_kernel(
         make_identity(nc, ident_f[:], nomemset=True)
         rows_b = const.tile([P, P], BF16)
         nc.vector.memset(rows_b[:], 0.0)
-        zrow = const.tile([P, 1024], BF16)
+        zrow = const.tile([P, E * OD], BF16)
         nc.vector.memset(zrow[:], 0.0)
         ones = const.tile([P, P], BF16)
         nc.vector.memset(ones[:], 1.0)
@@ -139,19 +139,16 @@ def tile_ensembleenvprob_pa_kernel(
             nc.scalar.copy(out=cols_a[:], in_=tl["rows_ps"][:, 0 : E * T])
 
         def sigma_vectors():
-            bc_ps = ps_2.tile([P, 1024], BF16, name="bc_ps", tag="sg")
-            for k in range(2):
+            bc_ps = ps_1.tile([P, E * OD], BF16, name="bc_ps", tag="s1")
+            tl["bc_ps"] = bc_ps
+            for k0 in (0, 448):
                 nc.tensor.matmul(
-                    out=bc_ps[:, 512 * k : 512 * (k + 1)], lhsT=ones[:],
-                    rhs=zrow[:, 512 * k : 512 * (k + 1)], start=True, stop=True,
+                    out=bc_ps[:, k0 : k0 + 448], lhsT=ones[:], rhs=zrow[:, k0 : k0 + 448],
+                    start=True, stop=True,
                 )
             rows_ps = ps_2.tile([P, P], BF16, name="rows_b_ps", tag="mu")
             nc.tensor.transpose(rows_ps[:], rows_b[:], ident_b[:])
             nc.scalar.copy(out=cols_b[:], in_=rows_ps[:, 0:12])
-            for k in range(2):
-                nc.scalar.copy(
-                    out=bmu_bc[:, 512 * k : 512 * (k + 1)], in_=bc_ps[:, 512 * k : 512 * (k + 1)]
-                )
 
         def tanh_constants():
             nc.vector.tensor_tensor(
@@ -175,7 +172,7 @@ def tile_ensembleenvprob_pa_kernel(
                 op0=ALU.mult, op1=ALU.add,
             )
 
-        bmu_bc = const.tile([P, 1024], BF16)
+        bmu_bc = const.tile([P, E * OD], BF16)
 
         mu_sb = res.tile([P, E, NCH, OD], F32)
         sg_s = res.tile([P, NCH, E, SD], F32)
@@ -317,11 +314,10 @@ def tile_ensembleenvprob_pa_kernel(
         wh_quant(0, 0, 256)
         wh_quant(0, 256, 512)
         wh_tiles(1)
-        wh_regroup(1, 0, 256, nc.vector.tensor_copy)
         h_quant(0, 0)
         h_quant(0, 1)
         bias_columns()
-        wh_regroup(1, 256, 512, nc.vector.tensor_copy)
+        wh_regroup(1, 0, HID, nc.vector.tensor_copy)
         wh_quant(1, 0, HID)
 
         stage1(0, lambda: h_transpose(1))
@@ -331,10 +327,15 @@ def tile_ensembleenvprob_pa_kernel(
 
         for i in range(1, E - 2):
             stage1(i, (lambda: tanh(i - 2)) if i > 1 else None)
+            h_transpose(i + 1)
             if i == 1:
                 sigma_vectors()
-            h_transpose(i + 1)
             w2_regroup(i)
+            if i == 1:
+                for k0 in (0, 448):
+                    nc.scalar.copy(
+                        out=bmu_bc[:, k0 : k0 + 448], in_=tl["bc_ps"][:, k0 : k0 + 448]
+                    )
             if i == E - 3:
                 h_transpose(E - 1)
                 w2_regroup(E - 2)
@@ -348,11 +349,11 @@ def tile_ensembleenvprob_pa_kernel(
             w2_quant(i - 1)
             stage2_sigma(i - 1)
             stage2_mu(i - 1)
-            if i == 1:
-                tanh_constants()
             wh_quant(i + 1, 0, HID)
             h_quant(i + 1, 0)
             h_quant(i + 1, 1)
+            if i == 1:
+                tanh_constants()
             if i == 2:
                 sqrt_constants()
             if i == E - 3:

@@ -62,7 +62,7 @@ def tile_ensembleenvprob_pa_kernel(
         nc.vector.memset(rows_b[:], 0.0)
         zrow = const.tile([P, E * OD], BF16)
         nc.vector.memset(zrow[:], 0.0)
-        ones = const.tile([P, P], BF16)
+        ones = const.tile([P, 512], BF16)
         nc.vector.memset(ones[:], 1.0)
         ident_b = const.tile([P, P], BF16)
 
@@ -143,7 +143,7 @@ def tile_ensembleenvprob_pa_kernel(
             tl["bc_ps"] = bc_ps
             for k0 in (0, 448):
                 nc.tensor.matmul(
-                    out=bc_ps[:, k0 : k0 + 448], lhsT=ones[:], rhs=zrow[:, k0 : k0 + 448],
+                    out=bc_ps[:, k0 : k0 + 448], lhsT=ones[:, 0:P], rhs=zrow[:, k0 : k0 + 448],
                     start=True, stop=True,
                 )
             rows_ps = ps_2.tile([P, P], BF16, name="rows_b_ps", tag="mu")
@@ -199,6 +199,13 @@ def tile_ensembleenvprob_pa_kernel(
                 rhs=rc[:, r0 : r0 + n].bitcast(FP8X4), rhs_scale=rs[:, r0 : r0 + n],
                 start=True, stop=True,
             )
+
+        def keep_clock(n):
+            for k in range(n):
+                idle = ps_1.tile([P, 512], F32, name="idle", tag="s1")
+                nc.tensor.matmul(
+                    out=idle[:], lhsT=ones[:, 0:P], rhs=ones[:], start=True, stop=True
+                )
 
         def h_transpose(e):
             t_a = ps_t.tile([P, 2, 2 * P], F32, name="t_a", tag="t")
@@ -309,6 +316,7 @@ def tile_ensembleenvprob_pa_kernel(
         wh_regroup(0, 0, 256, nc.vector.tensor_copy)
         wh_regroup(0, 256, 512, nc.vector.tensor_copy)
         nc.vector.tensor_copy(out=ident_b[:], in_=ident_f[:])
+        keep_clock(3)
         h_transpose(0)
         bias_transpose()
         wh_quant(0, 0, 256)
@@ -328,6 +336,7 @@ def tile_ensembleenvprob_pa_kernel(
         for i in range(1, E - 2):
             stage1(i, (lambda: tanh(i - 2)) if i > 1 else None)
             h_transpose(i + 1)
+            keep_clock(1)
             if i == 1:
                 sigma_vectors()
             w2_regroup(i)
@@ -375,6 +384,7 @@ def tile_ensembleenvprob_pa_kernel(
             stage2_sigma(i)
             if i < E - 1:
                 stage2_mu(i)
+                keep_clock(1)
                 tanh(i)
 
         tp = {}
@@ -408,20 +418,20 @@ def tile_ensembleenvprob_pa_kernel(
                 )
                 nc.sync.dma_start(out=o1[:, c, e0:e1, :], in_=sg_s[:, c, e0:e1, :])
 
-        variance(0, 4)
-        turn(0)
         mu_out(E - 4)
         stage2_mu(E - 1)
+        variance(0, 4)
+        turn(0)
+        mu_out(E - 1)
         mu_out(E - 3)
         mu_out(E - 2)
         tanh(E - 1)
         variance(4, E - 1)
         variance(E - 1, E)
         turn(1)
-        root(0)
-        mu_out(E - 1)
         nc.vector.tensor_copy(
             out=mu_r[:].rearrange("p c e o -> p e c o"), in_=mu_sb[:, :, :, SD:OD]
         )
         nc.sync.dma_start(out=o2, in_=mu_r[:])
+        root(0)
         root(1)

@@ -62,7 +62,7 @@ def tile_ensembleenvprob_pa_kernel(
         nc.vector.memset(rows_b[:], 0.0)
         zrow = const.tile([P, E * OD], BF16)
         nc.vector.memset(zrow[:], 0.0)
-        ones = const.tile([P, 512], BF16)
+        ones = const.tile([P, P], BF16)
         nc.vector.memset(ones[:], 1.0)
         ident_b = const.tile([P, P], BF16)
 
@@ -143,7 +143,7 @@ def tile_ensembleenvprob_pa_kernel(
             tl["bc_ps"] = bc_ps
             for k0 in (0, 448):
                 nc.tensor.matmul(
-                    out=bc_ps[:, k0 : k0 + 448], lhsT=ones[:, 0:P], rhs=zrow[:, k0 : k0 + 448],
+                    out=bc_ps[:, k0 : k0 + 448], lhsT=ones[:], rhs=zrow[:, k0 : k0 + 448],
                     start=True, stop=True,
                 )
             rows_ps = ps_2.tile([P, P], BF16, name="rows_b_ps", tag="mu")
@@ -200,12 +200,9 @@ def tile_ensembleenvprob_pa_kernel(
                 start=True, stop=True,
             )
 
-        def keep_clock(n):
-            for k in range(n):
-                idle = ps_1.tile([P, 512], F32, name="idle", tag="s1")
-                nc.tensor.matmul(
-                    out=idle[:], lhsT=ones[:, 0:P], rhs=ones[:], start=True, stop=True
-                )
+        def keep_clock(moving):
+            idle = ps_1.tile([P, 512], F32, name="idle", tag="s1")
+            nc.tensor.matmul(out=idle[:], lhsT=ones[:], rhs=moving, start=True, stop=True)
 
         def h_transpose(e):
             t_a = ps_t.tile([P, 2, 2 * P], F32, name="t_a", tag="t")
@@ -316,9 +313,11 @@ def tile_ensembleenvprob_pa_kernel(
         wh_regroup(0, 0, 256, nc.vector.tensor_copy)
         wh_regroup(0, 256, 512, nc.vector.tensor_copy)
         nc.vector.tensor_copy(out=ident_b[:], in_=ident_f[:])
-        keep_clock(3)
+        for t in range(2):
+            keep_clock(wh_raw[:, 0, t, :])
         h_transpose(0)
         bias_transpose()
+        keep_clock(wh_raw[:, 0, 2, :])
         wh_quant(0, 0, 256)
         wh_quant(0, 256, 512)
         wh_tiles(1)
@@ -329,6 +328,7 @@ def tile_ensembleenvprob_pa_kernel(
         wh_quant(1, 0, HID)
 
         stage1(0, lambda: h_transpose(1))
+        keep_clock(wh_raw[:, 0, 3, :])
         h_quant(1, 0)
         h_quant(1, 1)
         w2_regroup(0)
@@ -336,7 +336,6 @@ def tile_ensembleenvprob_pa_kernel(
         for i in range(1, E - 2):
             stage1(i, (lambda: tanh(i - 2)) if i > 1 else None)
             h_transpose(i + 1)
-            keep_clock(1)
             if i == 1:
                 sigma_vectors()
             w2_regroup(i)
@@ -356,6 +355,7 @@ def tile_ensembleenvprob_pa_kernel(
                 mu_out(i - 2)
             g_quant(i - 1)
             w2_quant(i - 1)
+            keep_clock(tl["wg", i + 1][:, 0:512])
             stage2_sigma(i - 1)
             stage2_mu(i - 1)
             wh_quant(i + 1, 0, HID)
@@ -384,7 +384,7 @@ def tile_ensembleenvprob_pa_kernel(
             stage2_sigma(i)
             if i < E - 1:
                 stage2_mu(i)
-                keep_clock(1)
+                keep_clock(wh_raw[:, i, 0, :])
                 tanh(i)
 
         tp = {}

@@ -94,7 +94,8 @@ def tile_ensembleenvprob_pa_kernel(
 
         load_wh(0)
         nc.sync.dma_start(out=rows_a[0 : E * T, :], in_=bh.rearrange("e (t p) -> (e t) p", p=P))
-        load_h(0, 1)
+        for c0, c1 in ((0, 2), (2, NCH)):
+            nc.sync.dma_start(out=h_raw[0][0][:, c0:c1], in_=h_view[:, c0:c1, 0:HID])
         warm = const.tile([P, 2], F32)
         nc.scalar.activation(out=warm[:], in_=twos[:], func=ACT.Silu)
         load_wh(1)
@@ -219,7 +220,8 @@ def tile_ensembleenvprob_pa_kernel(
                 out=hg_words[:, 0:512].rearrange("p (n u) -> p n u", u=2),
                 in_=t_a[:].rearrange("p u n -> p n u"),
             )
-            nc.scalar.copy(
+            copy_b = nc.vector.tensor_copy if e < 2 else nc.scalar.copy
+            copy_b(
                 out=hg_words[:, 512:768].rearrange("p (n u) -> p n u", u=2),
                 in_=t_b[:].rearrange("p u n -> p n u"),
             )
@@ -315,22 +317,22 @@ def tile_ensembleenvprob_pa_kernel(
         nc.vector.tensor_copy(out=ident_b[:], in_=ident_f[:])
         for t in range(2):
             keep_clock(wh_raw[:, 0, t, :])
+        wh_quant(0, 0, 256)
+        wh_quant(0, 256, 512)
         h_transpose(0)
         bias_transpose()
         keep_clock(wh_raw[:, 0, 2, :])
-        wh_quant(0, 0, 256)
-        wh_quant(0, 256, 512)
         wh_tiles(1)
-        h_quant(0, 0)
         h_quant(0, 1)
+        h_quant(0, 0)
         bias_columns()
         wh_regroup(1, 0, HID, nc.vector.tensor_copy)
         wh_quant(1, 0, HID)
 
         stage1(0, lambda: h_transpose(1))
         keep_clock(wh_raw[:, 0, 3, :])
-        h_quant(1, 0)
         h_quant(1, 1)
+        h_quant(1, 0)
         w2_regroup(0)
 
         for i in range(1, E - 2):
@@ -340,10 +342,7 @@ def tile_ensembleenvprob_pa_kernel(
                 sigma_vectors()
             w2_regroup(i)
             if i == 1:
-                for k0 in (0, 448):
-                    nc.scalar.copy(
-                        out=bmu_bc[:, k0 : k0 + 448], in_=tl["bc_ps"][:, k0 : k0 + 448]
-                    )
+                nc.scalar.copy(out=bmu_bc[:], in_=tl["bc_ps"][:])
             if i == E - 3:
                 h_transpose(E - 1)
                 w2_regroup(E - 2)
@@ -363,8 +362,6 @@ def tile_ensembleenvprob_pa_kernel(
             h_quant(i + 1, 1)
             if i == 1:
                 tanh_constants()
-            if i == 2:
-                sqrt_constants()
             if i == E - 3:
                 wh_tiles(E - 1)
                 wh_regroup(E - 1, 0, HID, nc.vector.tensor_copy)
@@ -420,6 +417,7 @@ def tile_ensembleenvprob_pa_kernel(
 
         mu_out(E - 4)
         stage2_mu(E - 1)
+        sqrt_constants()
         variance(0, 4)
         turn(0)
         mu_out(E - 1)

from contextlib import ExitStack

import concourse.mybir as mybir
from concourse.masks import make_identity

F32 = mybir.dt.float32
BF16 = mybir.dt.bfloat16
U32 = mybir.dt.uint32
U8 = mybir.dt.uint8
FP8X4 = mybir.dt.float8_e4m3fn_x4
ACT = mybir.ActivationFunctionType
ALU = mybir.AluOpType

P = 128
N_ROWS = 384
NCH = N_ROWS // P
E = 7
HID = 512
OD = 128
SD = 120
RD = 8
T = 4
LOG2_E = 1.4426950408889634

FLOPS = 2 * E * N_ROWS * HID * (HID + 2 * OD)

HALVES = ((0, 4), (4, E))
H_GROUPS = ((0, 1), (1, 2), (2, 3), (3, 5), (5, 7))


def regroup(engine_copy, dst, src):
    engine_copy(
        out=dst.rearrange("p (c i t) -> p c t i", i=4, t=T),
        in_=src.rearrange("p t (c i) -> p c t i", i=4),
    )


def tile_ensembleenvprob_pa_kernel(
    tc, h, Wh, bh, Wmu, bmu, Wsig, bsig, max_lv_s, min_lv_s, max_lv_r, min_lv_r,
    out_0, out_1, out_2, out_3,
):
    nc = tc.nc
    with ExitStack() as ctx:
        const = ctx.enter_context(tc.tile_pool(name="const", bufs=1))
        raw = ctx.enter_context(tc.tile_pool(name="raw", bufs=1))
        grp = ctx.enter_context(tc.tile_pool(name="grp", bufs=3))
        cod = ctx.enter_context(tc.tile_pool(name="cod", bufs=4))
        res = ctx.enter_context(tc.tile_pool(name="res", bufs=1))
        ps_t = ctx.enter_context(tc.psum_pool(name="ps_t", bufs=2))
        ps_1 = ctx.enter_context(tc.psum_pool(name="ps_1", bufs=4))
        ps_2 = ctx.enter_context(tc.psum_pool(name="ps_2", bufs=1))
        ctx.enter_context(tc.manual_schedule())

        twos = const.tile([P, 2], F32)
        nc.vector.memset(twos[:], 2.0)
        rows_a = const.tile([P, P], BF16)
        nc.vector.memset(rows_a[:], 0.0)
        ident_f = const.tile([P, P], F32)
        nc.vector.memset(ident_f[:], 0.0)
        make_identity(nc, ident_f[:], nomemset=True)
        rows_b = const.tile([P, P], BF16)
        nc.vector.memset(rows_b[:], 0.0)
        zrow = const.tile([P, E * OD], BF16)
        nc.vector.memset(zrow[:], 0.0)
        ones = const.tile([P, P], BF16)
        nc.vector.memset(ones[:], 1.0)
        ident_b = const.tile([P, P], BF16)

        h_raw = {}
        for g0, g1 in H_GROUPS:
            hr = raw.tile([P, NCH, (g1 - g0) * HID], BF16, name="h_raw%d" % g0, tag="h_raw%d" % g0)
            for e in range(g0, g1):
                h_raw[e] = (hr, e - g0)
        wh_raw = raw.tile([P, E, T, HID], BF16)
        w2_raw = raw.tile([P, E, T, 2 * OD], BF16)
        h_view = h.rearrange("(c p) e k -> p c (e k)", p=P)

        def load_h(e0, e1):
            nc.sync.dma_start(out=h_raw[e0][0][:], in_=h_view[:, :, e0 * HID : e1 * HID])

        def load_wh(e):
            nc.sync.dma_start(
                out=wh_raw[:, e].rearrange("p (u r) j -> p u (r j)", u=2),
                in_=Wh[e].rearrange("(u p r) j -> p u (r j)", u=2, p=P, r=2),
            )

        def load_w2(e0, e1):
            for e in range(e0, e1):
                for i, w in enumerate((Wmu, Wsig)):
                    nc.sync.dma_start(
                        out=w2_raw[:, e, :, i * OD : (i + 1) * OD],
                        in_=w[e].rearrange("(t p) o -> p t o", p=P),
                    )

        load_wh(0)
        nc.sync.dma_start(out=rows_a[0 : E * T, :], in_=bh.rearrange("e (t p) -> (e t) p", p=P))
        for c0, c1 in ((0, 2), (2, NCH)):
            nc.sync.dma_start(out=h_raw[0][0][:, c0:c1], in_=h_view[:, c0:c1, 0:HID])
        warm = const.tile([P, 2], F32)
        nc.scalar.activation(out=warm[:], in_=twos[:], func=ACT.Silu)
        load_wh(1)
        load_h(1, 2)
        load_w2(0, 1)
        load_wh(2)
        load_h(2, 3)
        nc.sync.dma_start(out=rows_b[0:E, :], in_=bsig)
        nc.sync.dma_start(out=rows_b[8:9, 0:SD], in_=max_lv_s)
        nc.sync.dma_start(out=rows_b[9:10, 0:SD], in_=min_lv_s)
        nc.sync.dma_start(out=rows_b[10:11, SD:OD], in_=max_lv_r)
        nc.sync.dma_start(out=rows_b[11:12, SD:OD], in_=min_lv_r)
        nc.sync.dma_start(
            out=zrow[0:1, 0 : E * OD], in_=bmu.rearrange("e o -> (e o)").unsqueeze(0)
        )
        load_w2(1, 2)
        load_wh(3)
        load_h(3, 5)
        load_w2(2, 3)
        load_wh(4)
        load_w2(3, 4)
        load_wh(5)
        load_h(5, 7)
        load_w2(4, 5)
        load_wh(6)
        load_w2(5, 7)

        cols_a = const.tile([P, E * T], F32)
        cols_b = const.tile([P, 12], F32)
        hl = const.tile([P, 2], F32)
        hl2 = const.tile([P, 2], F32)
        ehl = const.tile([P, 2], F32)
        half_a = const.tile([P, 1], F32)
        sq_bias = const.tile([P, 1], F32)
        th_bias = const.tile([P, E], F32)

        def bias_transpose():
            tl["rows_ps"] = ps_2.tile([P, P], BF16, name="rows_a_ps", tag="mu")
            nc.tensor.transpose(tl["rows_ps"][:], rows_a[:], ident_b[:])

        def bias_columns():
            nc.scalar.copy(out=cols_a[:], in_=tl["rows_ps"][:, 0 : E * T])

        def sigma_vectors():
            bc_ps = ps_1.tile([P, E * OD], BF16, name="bc_ps", tag="s1")
            tl["bc_ps"] = bc_ps
            for k0 in (0, 448):
                nc.tensor.matmul(
                    out=bc_ps[:, k0 : k0 + 448], lhsT=ones[:], rhs=zrow[:, k0 : k0 + 448],
                    start=True, stop=True,
                )
            rows_ps = ps_2.tile([P, P], BF16, name="rows_b_ps", tag="mu")
            nc.tensor.transpose(rows_ps[:], rows_b[:], ident_b[:])
            nc.scalar.copy(out=cols_b[:], in_=rows_ps[:, 0:12])

        def tanh_constants():
            nc.vector.tensor_tensor(
                out=hl[:], in0=cols_b[:, 8:10], in1=cols_b[:, 10:12], op=ALU.add
            )
            nc.vector.tensor_scalar(
                out=hl2[:], in0=hl[:], scalar1=LOG2_E, scalar2=None, op0=ALU.mult
            )
            nc.gpsimd.tensor_tensor(out=ehl[:], in0=twos[:], in1=hl2[:], op=ALU.pow)
            nc.vector.scalar_tensor_tensor(
                out=th_bias[:], in0=hl[:, 0:1].to_broadcast([P, E]), scalar=-0.5,
                in1=cols_b[:, 0:E], op0=ALU.mult, op1=ALU.add,
            )

        def sqrt_constants():
            nc.vector.tensor_scalar(
                out=half_a[:], in0=ehl[:, 0:1], scalar1=0.5, scalar2=None, op0=ALU.mult
            )
            nc.vector.scalar_tensor_tensor(
                out=sq_bias[:], in0=ehl[:, 0:1], scalar=0.5, in1=ehl[:, 1:2],
                op0=ALU.mult, op1=ALU.add,
            )

        bmu_bc = const.tile([P, E * OD], BF16)

        mu_sb = res.tile([P, E, NCH, OD], F32)
        sg_s = res.tile([P, NCH, E, SD], F32)
        sg_r = res.tile([P, NCH, E, RD], F32)
        th = res.tile([P, E, N_ROWS], F32)
        mu_r = res.tile([P, NCH, E, RD], F32)
        o0 = out_0.rearrange("(c p) e o -> p c e o", p=P)
        o1 = out_1.rearrange("(c p) e o -> p c e o", p=P)
        o2 = out_2.rearrange("(c p) e o -> p c e o", p=P)
        o3 = out_3.rearrange("(c p) e o -> p c e o", p=P)

        tl = {}

        def quant(codes, scales, grouped, w0, w1):
            nc.vector.quantize_mx(
                out=codes[:, w0:w1].bitcast(FP8X4), scales=scales[:, w0:w1],
                in_=grouped[:, T * w0 : T * w1],
            )

        def mx(out, lc, ls, l0, rc, rs, r0, n):
            nc.tensor.matmul_mx(
                out=out,
                lhsT=lc[:, l0 : l0 + P].bitcast(FP8X4), lhsT_scale=ls[:, l0 : l0 + P],
                rhs=rc[:, r0 : r0 + n].bitcast(FP8X4), rhs_scale=rs[:, r0 : r0 + n],
                start=True, stop=True,
            )

        def keep_clock(moving):
            idle = ps_1.tile([P, 512], F32, name="idle", tag="s1")
            nc.tensor.matmul(out=idle[:], lhsT=ones[:], rhs=moving, start=True, stop=True)

        def h_transpose(e):
            t_a = ps_t.tile([P, 2, 2 * P], F32, name="t_a", tag="t")
            t_b = ps_t.tile([P, 2, P], F32, name="t_b", tag="t")
            h_words = h_raw[e][0][:].bitcast(F32)
            for c in range(NCH):
                for u in range(2):
                    dst = t_a[:, u, c * P : (c + 1) * P] if c < 2 else t_b[:, u, :]
                    w0 = h_raw[e][1] * (HID // 2) + u * P
                    nc.tensor.transpose(dst, h_words[:, c, w0 : w0 + P], ident_f[:])
            hg = grp.tile([P, T * N_ROWS], BF16, name="hg", tag="hg", align_bytes=64)
            hg_words = hg[:].bitcast(F32)
            nc.scalar.copy(
                out=hg_words[:, 0:512].rearrange("p (n u) -> p n u", u=2),
                in_=t_a[:].rearrange("p u n -> p n u"),
            )
            copy_b = nc.vector.tensor_copy if e < 2 else nc.scalar.copy
            copy_b(
                out=hg_words[:, 512:768].rearrange("p (n u) -> p n u", u=2),
                in_=t_b[:].rearrange("p u n -> p n u"),
            )
            tl["hg", e] = hg
            tl["hc", e] = cod.tile([P, N_ROWS], U32, name="hc", tag="hc", align_bytes=64)
            tl["hs", e] = cod.tile([P, N_ROWS], U8, name="hs", tag="hs", align_bytes=64)

        def h_quant(e, part):
            w0, w1 = ((0, 256), (256, 384))[part]
            quant(tl["hc", e], tl["hs", e], tl["hg", e], w0, w1)

        def wh_tiles(e):
            tl["wg", e] = grp.tile([P, T * HID], BF16, name="wg", tag="wg", align_bytes=64)
            tl["wc", e] = cod.tile([P, HID], U32, name="wc", tag="wc", align_bytes=64)
            tl["ws", e] = cod.tile([P, HID], U8, name="ws", tag="ws", align_bytes=64)

        def wh_regroup(e, j0, j1, engine_copy):
            regroup(engine_copy, tl["wg", e][:, T * j0 : T * j1], wh_raw[:, e, :, j0:j1])

        def wh_quant(e, j0, j1):
            quant(tl["wc", e], tl["ws", e], tl["wg", e], j0, j1)

        def stage1(e, between=None):
            g_t = grp.tile([P, T, N_ROWS], BF16, name="g_t", tag="g_t")
            tl["g_t", e] = g_t
            wc, ws, hc, hs = tl["wc", e], tl["ws", e], tl["hc", e], tl["hs", e]
            for t in range(T):
                s1 = ps_1.tile([P, N_ROWS], F32, name="s1", tag="s1")
                mx(s1[:, 0:256], wc, ws, t * P, hc, hs, 0, 256)
                mx(s1[:, 256:384], wc, ws, t * P, hc, hs, 256, 128)
                nc.scalar.activation(
                    out=g_t[:, t, :], in_=s1[:], func=ACT.Silu,
                    bias=cols_a[:, T * e + t : T * e + t + 1], scale=1.0,
                )
                if t == 1 and between is not None:
                    between()

        def w2_regroup(e, engine_copy=nc.scalar.copy):
            w2g = grp.tile([P, T * 2 * OD], BF16, name="w2g", tag="w2g", align_bytes=64)
            tl["w2g", e] = w2g
            regroup(engine_copy, w2g[:], w2_raw[:, e])

        def g_regroup(e):
            gg = grp.tile([P, T * N_ROWS], BF16, name="gg", tag="gg", align_bytes=64)
            tl["gg", e] = gg
            regroup(nc.vector.tensor_copy, gg[:], tl["g_t", e][:])

        def g_tiles(e):
            tl["gc", e] = cod.tile([P, N_ROWS], U32, name="gc", tag="gc", align_bytes=64)
            tl["gs", e] = cod.tile([P, N_ROWS], U8, name="gs", tag="gs", align_bytes=64)
            tl["w2c", e] = cod.tile([P, 2 * OD], U32, name="w2c", tag="w2c", align_bytes=64)
            tl["w2s", e] = cod.tile([P, 2 * OD], U8, name="w2s", tag="w2s", align_bytes=64)

        def g_quant(e):
            quant(tl["gc", e], tl["gs", e], tl["gg", e], 0, 256)
            quant(tl["gc", e], tl["gs", e], tl["gg", e], 256, 384)

        def w2_quant(e):
            quant(tl["w2c", e], tl["w2s", e], tl["w2g", e], 0, 2 * OD)

        def stage2_sigma(e):
            gc, gs, w2c, w2s = tl["gc", e], tl["gs", e], tl["w2c", e], tl["w2s", e]
            sg_ps = ps_2.tile([P, N_ROWS], F32, name="sg_ps", tag="sg")
            mx(sg_ps[:, 0:256], w2c, w2s, OD, gc, gs, 0, 256)
            mx(sg_ps[:, 256:384], w2c, w2s, OD, gc, gs, 256, 128)
            tl["sg_ps", e] = sg_ps

        def stage2_mu(e):
            gc, gs, w2c, w2s = tl["gc", e], tl["gs", e], tl["w2c", e], tl["w2s", e]
            pool, tag = (ps_t, "t") if e in (E - 3, E - 2) else (ps_2, "mu")
            mu_ps = pool.tile([P, NCH, OD], F32, name="mu_ps", tag=tag)
            for c in range(NCH):
                mx(mu_ps[:, c, :], gc, gs, c * P, w2c, w2s, 0, OD)
            tl["mu_ps", e] = mu_ps

        def tanh(e):
            nc.scalar.activation(
                out=th[:, e, :], in_=tl["sg_ps", e][:], func=ACT.Tanh,
                bias=th_bias[:, e : e + 1], scale=1.0,
            )

        def mu_out(e):
            nc.vector.tensor_tensor(
                out=mu_sb[:, e], in0=tl["mu_ps", e][:],
                in1=bmu_bc[:, e * OD : (e + 1) * OD].unsqueeze(1).to_broadcast([P, NCH, OD]),
                op=ALU.add,
            )
            nc.sync.dma_start(out=o0[:, :, e, :], in_=mu_sb[:, e, :, 0:SD])

        wh_tiles(0)
        wh_regroup(0, 0, 256, nc.vector.tensor_copy)
        wh_regroup(0, 256, 512, nc.vector.tensor_copy)
        nc.vector.tensor_copy(out=ident_b[:], in_=ident_f[:])
        for t in range(2):
            keep_clock(wh_raw[:, 0, t, :])
        wh_quant(0, 0, 256)
        wh_quant(0, 256, 512)
        h_transpose(0)
        bias_transpose()
        keep_clock(wh_raw[:, 0, 2, :])
        wh_tiles(1)
        h_quant(0, 1)
        h_quant(0, 0)
        bias_columns()
        wh_regroup(1, 0, HID, nc.vector.tensor_copy)
        wh_quant(1, 0, HID)

        stage1(0, lambda: h_transpose(1))
        keep_clock(wh_raw[:, 0, 3, :])
        h_quant(1, 1)
        h_quant(1, 0)
        w2_regroup(0)

        for i in range(1, E - 2):
            stage1(i, (lambda: tanh(i - 2)) if i > 1 else None)
            h_transpose(i + 1)
            if i == 1:
                sigma_vectors()
            w2_regroup(i)
            if i == 1:
                nc.scalar.copy(out=bmu_bc[:], in_=tl["bc_ps"][:])
            if i == E - 3:
                h_transpose(E - 1)
                w2_regroup(E - 2)
            g_regroup(i - 1)
            g_tiles(i - 1)
            wh_tiles(i + 1)
            wh_regroup(i + 1, 0, HID, nc.vector.tensor_copy)
            if i > 1:
                mu_out(i - 2)
            g_quant(i - 1)
            w2_quant(i - 1)
            keep_clock(tl["wg", i + 1][:, 0:512])
            stage2_sigma(i - 1)
            stage2_mu(i - 1)
            wh_quant(i + 1, 0, HID)
            h_quant(i + 1, 0)
            h_quant(i + 1, 1)
            if i == 1:
                tanh_constants()
            if i == E - 3:
                wh_tiles(E - 1)
                wh_regroup(E - 1, 0, HID, nc.vector.tensor_copy)

        stage1(E - 2, lambda: tanh(E - 4))
        h_quant(E - 1, 0)
        h_quant(E - 1, 1)
        wh_quant(E - 1, 0, HID)
        stage1(E - 1)
        for i in range(E - 3, E):
            g_tiles(i)
            g_regroup(i)
            if i == E - 2:
                w2_regroup(E - 1, nc.vector.tensor_copy)
            w2_quant(i)
            g_quant(i)
            stage2_sigma(i)
            if i < E - 1:
                stage2_mu(i)
                keep_clock(wh_raw[:, i, 0, :])
                tanh(i)

        tp = {}

        def variance(e0, e1):
            nc.vector.tensor_scalar(
                out=th[:, e0:e1, :], in0=th[:, e0:e1, :], scalar1=half_a[:, 0:1],
                scalar2=sq_bias[:, 0:1], op0=ALU.mult, op1=ALU.add,
            )

        def turn(half):
            e0, e1 = HALVES[half]
            for c in range(NCH):
                pool, tag = (ps_t, "t") if half == 1 and c > 0 else (ps_1, "s1")
                tp[half, c] = pool.tile([P, 4, OD], F32, name="tp", tag=tag)
                for e in range(e0, e1):
                    nc.tensor.transpose(
                        tp[half, c][:, e - e0, :], th[:, e, c * P : (c + 1) * P], ident_f[:]
                    )

        def root(half):
            e0, e1 = HALVES[half]
            for c in range(NCH):
                nc.scalar.activation(
                    out=sg_r[:, c, e0:e1, :], in_=tp[half, c][:, 0 : e1 - e0, SD:OD], func=ACT.Sqrt
                )
                if half == 1 and c == NCH - 1:
                    nc.sync.dma_start(out=o3, in_=sg_r[:])
                nc.scalar.activation(
                    out=sg_s[:, c, e0:e1, :], in_=tp[half, c][:, 0 : e1 - e0, 0:SD], func=ACT.Sqrt
                )
                nc.sync.dma_start(out=o1[:, c, e0:e1, :], in_=sg_s[:, c, e0:e1, :])

        mu_out(E - 4)
        stage2_mu(E - 1)
        sqrt_constants()
        variance(0, 4)
        turn(0)
        mu_out(E - 1)
        mu_out(E - 3)
        mu_out(E - 2)
        tanh(E - 1)
        variance(4, E - 1)
        variance(E - 1, E)
        turn(1)
        nc.vector.tensor_copy(
            out=mu_r[:].rearrange("p c e o -> p e c o"), in_=mu_sb[:, :, :, SD:OD]
        )
        nc.sync.dma_start(out=o2, in_=mu_r[:])
        root(0)
        root(1)
